import numpy as np
import ml_dtypes


def mxq(x, axis, fmt="e4m3"):
    dtype, down = {"e4m3": (ml_dtypes.float8_e4m3fn, 7), "e5m2": (ml_dtypes.float8_e5m2, 14)}[fmt]
    v = np.moveaxis(np.asarray(x, np.float32).astype(ml_dtypes.bfloat16).astype(np.float64), axis, -1)
    blocks = v.reshape(v.shape[:-1] + (-1, 32))
    amax = np.abs(blocks).max(-1, keepdims=True)
    byte = np.maximum(np.where(amax > 0, np.frexp(amax)[1] - 1 + 127, 0) - down, 1)
    scale = np.exp2(byte - 127.0)
    codes = (blocks / scale).astype(np.float32).astype(dtype).astype(np.float64)
    return np.moveaxis((codes * scale).reshape(v.shape), -1, axis)


WIDE = False


def mx_kscale(k):
    if not WIDE:
        return np.ones(k)
    levels = np.array([10, -10, 5, -5, 0])
    if k % 512:
        return np.exp2(np.random.permutation(np.resize(levels, k // 32))).repeat(32)
    a = np.empty((k // 512, 16))
    for p in range(k // 512):
        a[p, :8] = np.random.permutation(np.resize(levels, 8))
        for g in range(8):
            far = levels[np.abs(levels - a[p, g]) >= 10]
            a[p, g + 8] = far[np.random.randint(len(far))]
    return np.exp2(a.ravel()).repeat(32)


BF16 = ml_dtypes.bfloat16


def bf(x):
    return np.asarray(x, np.float32).astype(BF16)


def f64(x):
    return np.asarray(x).astype(np.float64)


E2M1 = np.array([0.0, 0.5, 1.0, 1.5, 2.0, 3.0, 4.0, 6.0, -0.0, -0.5, -1.0, -1.5, -2.0, -3.0, -4.0, -6.0])


def pack_weight(w, fmt):
    k, n = w.shape
    w = f64(bf(w)).reshape(k // 32, 32, n)
    amax = np.abs(w).max(1)
    if fmt == "e4m3":
        byte = np.frexp(amax)[1] - 1 + 127 - 7
    else:
        mant, ex = np.frexp(amax / 6.0)
        byte = np.where(mant > 0.5, ex, ex - 1) + 127
    byte = np.clip(np.where(amax > 0, byte, 1), 1, 254)
    scaled = (w * np.exp2(127.0 - byte)[:, None, :]).reshape(k, n).astype(np.float32)
    by_word = np.ascontiguousarray(scaled.reshape(k // 512, 128, 4, n).transpose(0, 1, 3, 2))
    if fmt == "e4m3":
        words = by_word.astype(ml_dtypes.float8_e4m3fn).view(np.uint8)
    else:
        c = by_word.astype(ml_dtypes.float4_e2m1fn).view(np.uint8) & 0xF
        words = c[..., 0::2] | (c[..., 1::2] << 4)
    return np.ascontiguousarray(words), np.ascontiguousarray(byte.astype(np.uint8).reshape(k // 512, 16, n))


def unpack_weight(words, scales, fmt):
    g, p, n, _ = words.shape
    if fmt == "e4m3":
        vals = np.ascontiguousarray(words).view(ml_dtypes.float8_e4m3fn).astype(np.float64)
    else:
        nib = np.empty((g, p, n, 4), np.uint8)
        nib[..., 0::2] = words & 0xF
        nib[..., 1::2] = words >> 4
        vals = E2M1[nib]
    vals = vals * np.repeat(np.exp2(scales.astype(np.float64) - 127.0), 8, axis=1)[..., None]
    return vals.transpose(0, 1, 3, 2).reshape(g * 512, n)
def pack4(w):
    words, scales = pack_weight(w, "e2m1")
    return words.reshape(words.shape[0], 128, -1), scales


def unpack4(words, scales):
    return unpack_weight(words.reshape(words.shape[0], 128, -1, 2), scales, "e2m1")


B, S, D, QL, KL, H = 2, 2048, 512, 512, 512, 4
HD = D // H
ROPE_BASE = 10000.0


def rope(x):
    d = x.shape[-1]
    half = d // 2
    inv_freq = 1.0 / (ROPE_BASE ** (np.arange(half, dtype=np.float64) * 2.0 / d))
    pos = np.arange(x.shape[1], dtype=np.float64)
    ang = pos[:, None] * inv_freq[None, :]
    cos = np.concatenate([np.cos(ang), np.cos(ang)], -1)[None]
    sin = np.concatenate([np.sin(ang), np.sin(ang)], -1)[None]
    x1, x2 = x[..., :half], x[..., half:]
    rot = np.concatenate([-x2, x1], -1)
    return x * cos + rot * sin


def draw0():
    s, t = mx_kscale(D), mx_kscale(QL)
    inputs_q = bf(np.random.standard_normal((B, S, D)) * s)
    down_words, down_scales = pack4(np.random.standard_normal((D, QL)) / np.sqrt(D) / s[:, None] * t)
    up_words, up_scales = pack4(np.random.standard_normal((QL, D)) / np.sqrt(QL) / t[:, None])
    rope_words, rope_scales = pack4(np.random.standard_normal((QL, D)) / np.sqrt(QL) / t[:, None])
    return {"inputs_q": inputs_q,
            "Wq_down_words": down_words, "Wq_down_scales": down_scales,
            "Wq_up_words": up_words, "Wq_up_scales": up_scales,
            "Wq_rope_words": rope_words, "Wq_rope_scales": rope_scales}


def core(inputs_q, Wq_down_words, Wq_down_scales, Wq_up_words, Wq_up_scales, Wq_rope_words, Wq_rope_scales):
    q_latent = mxq(f64(inputs_q), 2, "e4m3") @ unpack4(Wq_down_words, Wq_down_scales)
    lq = mxq(q_latent, 2, "e4m3")
    q_proj = (lq @ unpack4(Wq_up_words, Wq_up_scales)).reshape(B, S, H, HD)
    q_rope = rope(lq @ unpack4(Wq_rope_words, Wq_rope_scales)).reshape(B, S, H, HD)
    return np.concatenate([q_proj, q_rope], -1)


def e4m3fn_bytes(y):
    return np.clip(np.asarray(y, np.float64), -448.0, 448.0).astype(np.float32).astype(ml_dtypes.float8_e4m3fn).view(np.uint8)


def e4m3fn_values(b):
    return np.asarray(b, np.uint8).view(ml_dtypes.float8_e4m3fn).astype(np.float64)


def setup_inputs():
    d = draw0()
    x0 = np.asarray(d['inputs_q']).astype(np.float64)
    s = (np.max(np.abs(x0), axis=(0, 1), keepdims=True) / 448.0).astype(np.float32)
    out = {}
    for k, v in d.items():
        if k == 'inputs_q':
            out['inputs_q_bytes'] = e4m3fn_bytes(x0 / s.astype(np.float64))
            out['inputs_q_scale'] = s
        else:
            out[k] = v
    return out


def reference(inputs_q_bytes, inputs_q_scale, Wq_down_words, Wq_down_scales, Wq_up_words, Wq_up_scales, Wq_rope_words, Wq_rope_scales):
    return core(e4m3fn_values(inputs_q_bytes) * inputs_q_scale.astype(np.float64), Wq_down_words, Wq_down_scales, Wq_up_words, Wq_up_scales, Wq_rope_words, Wq_rope_scales)

@@ -1,0 +1,328 @@
+import math
+from contextlib import ExitStack
+
+import concourse.mybir as mybir
+from concourse.masks import make_identity
+
+B, S, D, H = 2, 2048, 512, 4
+P = 128
+HALF = D // 2
+FLOPS = 3 * 2 * B * S * D * D
+
+F32 = mybir.dt.float32
+BF16 = mybir.dt.bfloat16
+I32 = mybir.dt.int32
+U32 = mybir.dt.uint32
+U8 = mybir.dt.uint8
+FP8 = mybir.dt.float8_e4m3fn
+FP8X4 = mybir.dt.float8_e4m3fn_x4
+FP4X4 = mybir.dt.float4_e2m1fn_x4
+ALU = mybir.AluOpType
+ACT = mybir.ActivationFunctionType
+
+GROUPS = 4
+RHO = 10000.0 ** (-1.0 / HALF)
+TWO_PI = 2.0 * math.pi
+
+
+def reduced_columns(group):
+    last = 512 * group + 511
+    j = 0
+    while last * RHO**j > 3.1415:
+        j += 1
+    return (j + 7) // 8 * 8
+
+
+def tile_multiheadlatentattention_pa_t_w4_kernel(
+    tc, x_bytes, x_scale, down_words, down_scales, up_words, up_scales, rope_words, rope_scales, out
+):
+    nc = tc.nc
+    with ExitStack() as ctx:
+        keep = ctx.enter_context(tc.tile_pool(name="keep", bufs=1))
+        xin = ctx.enter_context(tc.tile_pool(name="xin", bufs=8))
+        work = ctx.enter_context(tc.tile_pool(name="work", bufs=3))
+        tabs = ctx.enter_context(tc.tile_pool(name="tabs", bufs=3))
+        outs = ctx.enter_context(tc.tile_pool(name="outs", bufs=4))
+        psum = ctx.enter_context(tc.psum_pool(name="psum", bufs=1))
+
+        scale_row = keep.tile([P, 2, D], F32, name="scale_row")
+        x_tiles = {}
+
+        def load_x(g, b):
+            t = xin.tile([P, 4 * D], U8, name="xb")
+            nc.sync.dma_start(
+                out=t[:], in_=x_bytes[b, 512 * g : 512 * g + 512, :].rearrange("(p i) k -> p (i k)", i=4)
+            )
+            x_tiles[(g, b)] = t
+
+        planes = keep.tile([P, 3, D], U8, name="planes", align_bytes=64)
+        nc.gpsimd.memset(planes[:].rearrange("p w n -> p (w n)").bitcast(I32), 0)
+
+        def load_scales(w, scales):
+            for q in range(4):
+                nc.sync.dma_start(
+                    out=planes[32 * q : 32 * q + 4, w, :].bitcast(I32),
+                    in_=scales[0, 4 * q : 4 * q + 4, :].bitcast(I32),
+                )
+
+        down_raw = keep.tile([P, 2 * D], U8, name="down_raw", align_bytes=64)
+        up_codes = keep.tile([P, 2 * D], U8, name="up_codes", align_bytes=64)
+        rope_codes = keep.tile([P, 2 * D], U8, name="rope_codes", align_bytes=64)
+        load_x(0, 0)
+        load_x(0, 1)
+        nc.sync.dma_start(out=scale_row[:, 0, :], in_=x_scale.rearrange("a o k -> (a o k)").partition_broadcast(P))
+        nc.sync.dma_start(out=down_raw[:], in_=down_words[0])
+        load_scales(0, down_scales)
+        nc.sync.dma_start(out=rope_codes[:], in_=rope_words[0])
+        load_scales(2, rope_scales)
+        nc.sync.dma_start(out=up_codes[:], in_=up_words[0])
+        load_scales(1, up_scales)
+        for g in range(GROUPS):
+            for b in range(B):
+                if g > 0:
+                    load_x(g, b)
+
+        dummy = keep.tile([P, 1], F32, name="dummy")
+        nc.vector.memset(dummy[:], 0.0)
+        nc.scalar.activation(out=dummy[:], in_=dummy[:], func=ACT.Sin)
+        pos = keep.tile([P, 4 * GROUPS], F32, name="pos")
+        nc.gpsimd.iota(
+            pos[:],
+            pattern=[[512, GROUPS], [1, 4]],
+            base=0,
+            channel_multiplier=4,
+            allow_small_or_imprecise_dtypes=True,
+        )
+        freq = keep.tile([P, HALF], F32, name="freq")
+        nc.vector.memset(freq[:], 1.0)
+        nc.vector.tensor_scalar(
+            out=freq[:, 0:1], in0=freq[:, 0:1], scalar1=1.0 / TWO_PI, scalar2=None, op0=ALU.mult
+        )
+        w = 1
+        while w < HALF:
+            nc.vector.tensor_scalar(
+                out=freq[:, w : 2 * w], in0=freq[:, 0:w], scalar1=RHO**w, scalar2=None, op0=ALU.mult
+            )
+            w *= 2
+        ident = keep.tile([P, P], F32, name="ident")
+        make_identity(nc, ident[:])
+        scale2 = scale_row[:].rearrange("p i k -> p (i k)")
+
+        turns = keep.tile([P, 4 * GROUPS, HALF], F32, name="turns")
+        whole = keep.tile([P, 4 * GROUPS, 192], I32, name="whole")
+
+        def raw_angles(eng, unit):
+            j0 = reduced_columns(unit // 2)
+            for c in (2 * unit, 2 * unit + 1):
+                eng.tensor_scalar(
+                    out=whole[:, c, 0:j0], in0=freq[:, 0:j0], scalar1=pos[:, c : c + 1], scalar2=0.0,
+                    op0=ALU.mult, op1=ALU.add,
+                )
+                eng.tensor_scalar(
+                    out=turns[:, c, :], in0=freq[:], scalar1=pos[:, c : c + 1], scalar2=0.0,
+                    op0=ALU.mult, op1=ALU.add,
+                )
+
+        def reduce_angles(first, last):
+            j0 = reduced_columns(first // 2)
+            part = turns[:, 2 * first : 2 * last, 0:j0]
+            nc.vector.tensor_tensor(out=part, in0=part, in1=whole[:, 2 * first : 2 * last, 0:j0], op=ALU.subtract)
+
+        tables = {}
+
+        def table_steps(unit):
+            j0 = reduced_columns(unit // 2)
+            sin_t = tabs.tile([P, 2, HALF], F32, name="sin_t")
+            mix_t = tabs.tile([P, 2, D], F32, name="mix_t")
+            a1 = tabs.tile([P, 2, 192], F32, name="a1")
+            a2 = tabs.tile([P, 2, 192], F32, name="a2")
+            tables[unit] = (sin_t, mix_t)
+            tu = turns[:, 2 * unit : 2 * unit + 2, :]
+            low, high = tu[:, :, 0:j0], tu[:, :, j0:HALF]
+
+            def act(o, i, f, bias, scale):
+                return lambda: nc.scalar.activation(out=o, in_=i, func=f, bias=bias, scale=scale)
+
+            q = math.pi / 4
+            return [
+                act(a1[:, :, 0:j0], low, ACT.Abs, -q, TWO_PI),
+                act(a2[:, :, 0:j0], low, ACT.Abs, q, TWO_PI),
+                act(mix_t[:, :, j0:HALF], high, ACT.Sin, 3 * q, -TWO_PI),
+                act(mix_t[:, :, 0:j0], a1[:, :, 0:j0], ACT.Sin, 2 * q, -1.0),
+                act(mix_t[:, :, HALF + j0 : D], high, ACT.Sin, q, -TWO_PI),
+                act(mix_t[:, :, HALF : HALF + j0], a2[:, :, 0:j0], ACT.Sin, 2 * q, -1.0),
+                act(sin_t[:], tu, ACT.Sin, 0.0, TWO_PI),
+            ]
+
+        down_codes = keep.tile([P, 4, 2 * P], U8, name="down_codes", align_bytes=64)
+        down_plane = keep.tile([P, 4, P], U8, name="down_plane", align_bytes=64)
+
+        chunks = [(g, b, h) for g in range(GROUPS) for h in range(2) for b in range(B)]
+        xw, xg, xq, lg, lq = {}, {}, {}, {}, {}
+
+        def widen(c):
+            g, b, h = chunks[c]
+            xw[c] = work.tile([P, 2 * D], BF16, name="xw", align_bytes=64)
+            nc.vector.tensor_tensor(
+                out=xw[c][:],
+                in0=x_tiles[(g, b)][:, 2 * D * h : 2 * D * (h + 1)].bitcast(FP8),
+                in1=scale2,
+                op=ALU.mult,
+            )
+
+        def turn(c):
+            words = xw[c][:].bitcast(F32)
+            bank = psum.tile([P, 2, 2, P], F32, name="xt_bank")
+            for i in range(2):
+                for u in range(2):
+                    nc.tensor.transpose(bank[:, i, u, :], words[:, 256 * i + u : 256 * (i + 1) : 2], ident[:])
+            xg[c] = work.tile([P, 4 * 256], BF16, name="xg", align_bytes=64)
+            nc.scalar.copy(
+                out=xg[c][:].bitcast(F32).rearrange("p (i r u) -> p i r u", i=2, u=2),
+                in_=bank[:].rearrange("p i u r -> p i r u"),
+            )
+
+        def quant(src, tag):
+            codes = work.tile([P, 256], U32, name=tag + "_codes", align_bytes=64)
+            plane = work.tile([P, 256], U8, name=tag + "_plane", align_bytes=64)
+            nc.vector.quantize_mx(out=codes[:].bitcast(FP8X4), scales=plane[:], in_=src[:])
+            return codes, plane
+
+        def latent(c):
+            codes, plane = xq[c]
+            lg[c] = work.tile([P, 4 * 256], BF16, name="lg", align_bytes=64)
+            for i in range(2):
+                cols = slice(P * i, P * (i + 1))
+                bank = psum.tile([P, 4, P], F32, name="lat_bank%d" % i)
+                for t in range(4):
+                    nc.tensor.matmul_mx(
+                        out=bank[:, t, :],
+                        lhsT=down_codes[:, t, :].bitcast(FP4X4),
+                        lhsT_scale=down_plane[:, t, :],
+                        rhs=codes[:, cols].bitcast(FP8X4),
+                        rhs_scale=plane[:, cols],
+                        start=True,
+                        stop=True,
+                    )
+                nc.scalar.copy(
+                    out=lg[c][:, 512 * i : 512 * (i + 1)].rearrange("p (n t) -> p n t", t=4),
+                    in_=bank[:].rearrange("p t n -> p n t"),
+                )
+
+        stages, mixes, sines, u_banks, q_banks = {}, {}, {}, {}, {}
+
+        def project(c):
+            codes, plane = lq[c]
+            stages[c] = outs.tile([P, 2, H, 256], F32, name="stage")
+            mixes[c] = work.tile([P, 2, D], F32, name="mixed")
+            sines[c] = work.tile([P, 2, HALF], F32, name="sined")
+            u_bank = psum.tile([P, 2, HALF], F32, name="u_bank")
+            g, b, h = chunks[c]
+
+            def mm(i, o, words, pl, a, n, start, stop):
+                cols = slice(P * i, P * (i + 1))
+                nc.tensor.matmul_mx(
+                    out=o,
+                    lhsT=codes[:, cols].bitcast(FP8X4),
+                    lhsT_scale=plane[:, cols],
+                    rhs=words[:, 2 * a : 2 * (a + n)].bitcast(FP4X4),
+                    rhs_scale=planes[:, pl, a : a + n],
+                    start=start,
+                    stop=stop,
+                )
+
+            for i in range(2):
+                r_bank = psum.tile([P, D], F32, name="r_bank%d" % i)
+                mm(i, r_bank[:], rope_codes, 2, 0, D, True, True)
+                nc.vector.scalar_tensor_tensor(
+                    out=mixes[c][:, i, :], in0=r_bank[:], scalar=math.sqrt(2.0), in1=tables[2 * g + h][1][:, i, :],
+                    op0=ALU.mult, op1=ALU.mult,
+                )
+            for i in range(2):
+                for half in range(2):
+                    mm(i, u_bank[:, i, P * half : P * (half + 1)], rope_codes, 2, P * half, P, True, False)
+                    mm(i, u_bank[:, i, P * half : P * (half + 1)], rope_codes, 2, HALF + P * half, P, False, True)
+            u_banks[c] = u_bank
+            for i in range(2):
+                q_bank = psum.tile([P, D], F32, name="q_bank%d" % i)
+                mm(i, q_bank[:], up_codes, 1, 0, D, True, True)
+                nc.scalar.copy(
+                    out=stages[c][:, i, :, 0:P], in_=q_bank[:].rearrange("p (h c) -> p h c", h=H)
+                )
+
+        def sine_part(c):
+            g, b, h = chunks[c]
+            nc.vector.tensor_tensor(
+                out=sines[c][:], in0=u_banks[c][:], in1=tables[2 * g + h][0][:], op=ALU.mult
+            )
+            nc.gpsimd.tensor_tensor(
+                out=stages[c][:, :, 2:4, P:256],
+                in0=mixes[c][:, :, HALF:D].rearrange("p i (h c) -> p i h c", h=2),
+                in1=sines[c][:].rearrange("p i (h c) -> p i h c", h=2),
+                op=ALU.add,
+            )
+
+        def first_half(c):
+            g, b, h = chunks[c]
+            nc.vector.tensor_tensor(
+                out=stages[c][:, :, 0:2, P:256],
+                in0=mixes[c][:, :, 0:HALF].rearrange("p i (h c) -> p i h c", h=2),
+                in1=sines[c][:].rearrange("p i (h c) -> p i h c", h=2),
+                op=ALU.subtract,
+            )
+            nc.sync.dma_start(
+                out=out[b, 512 * g : 512 * g + 512, :, :].rearrange("(p i) h c -> p i h c", i=4)[:, 2 * h : 2 * h + 2],
+                in_=stages[c][:],
+            )
+
+        def prepare_down():
+            nc.vector.tensor_copy(
+                out=down_codes[:].rearrange("p t (m b) -> p t m b", b=2),
+                in_=down_raw[:].rearrange("p (m t b) -> p t m b", t=4, b=2),
+            )
+            nc.vector.tensor_copy(
+                out=down_plane[:], in_=planes[:, 0, :].rearrange("p (m t) -> p t m", t=4)
+            )
+
+        n = len(chunks)
+        units = 2 * GROUPS
+        queue = []
+        with tc.manual_schedule():
+            raw_angles(nc.vector, 0)
+            for unit in range(1, units):
+                raw_angles(nc.gpsimd, unit)
+            reduce_angles(0, 1)
+            nc.scalar.copy(out=scale_row[:, 1, :], in_=scale_row[:, 0, :])
+            queued = 0
+            for k in range(-5, n + 1):
+                if 0 <= k < n:
+                    project(k)
+                if 0 <= k + 1 < n:
+                    lq[k + 1] = quant(lg[k + 1], "l")
+                if k == -3:
+                    prepare_down()
+                    reduce_angles(1, 2)
+                if k == -2:
+                    reduce_angles(2, 4)
+                if k == -1:
+                    reduce_angles(4, 6)
+                    reduce_angles(6, 8)
+                if 0 <= k + 3 < n:
+                    xq[k + 3] = quant(xg[k + 3], "x")
+                if 0 <= k + 5 < n:
+                    widen(k + 5)
+                if 0 <= k - 1 < n:
+                    first_half(k - 1)
+                if 0 <= k < n:
+                    sine_part(k)
+                if 0 <= k + 2 < n:
+                    latent(k + 2)
+                if 0 <= k + 4 < n:
+                    turn(k + 4)
+                take = 2 if k < 0 else 4
+                for i in range(take):
+                    if not queue and queued < units and 2 * queued <= k + 5:
+                        queue = table_steps(queued)
+                        queued += 1
+                    if queue:
+                        queue.pop(0)()

@@ -255,12 +255,6 @@ def tile_multiheadlatentattention_pa_t_w4_kernel(
             nc.vector.tensor_tensor(
                 out=sines[c][:], in0=u_banks[c][:], in1=tables[2 * g + h][0][:], op=ALU.mult
             )
-            nc.gpsimd.tensor_tensor(
-                out=stages[c][:, :, 2:4, P:256],
-                in0=mixes[c][:, :, HALF:D].rearrange("p i (h c) -> p i h c", h=2),
-                in1=sines[c][:].rearrange("p i (h c) -> p i h c", h=2),
-                op=ALU.add,
-            )
 
         def first_half(c):
             g, b, h = chunks[c]
@@ -269,6 +263,12 @@ def tile_multiheadlatentattention_pa_t_w4_kernel(
                 in0=mixes[c][:, :, 0:HALF].rearrange("p i (h c) -> p i h c", h=2),
                 in1=sines[c][:].rearrange("p i (h c) -> p i h c", h=2),
                 op=ALU.subtract,
+            )
+            nc.vector.tensor_tensor(
+                out=stages[c][:, :, 2:4, P:256],
+                in0=mixes[c][:, :, HALF:D].rearrange("p i (h c) -> p i h c", h=2),
+                in1=sines[c][:].rearrange("p i (h c) -> p i h c", h=2),
+                op=ALU.add,
             )
             nc.sync.dma_start(
                 out=out[b, 512 * g : 512 * g + 512, :, :].rearrange("(p i) h c -> p i h c", i=4)[:, 2 * h : 2 * h + 2],

@@ -20,6 +20,9 @@ FP4X4 = mybir.dt.float4_e2m1fn_x4
 ALU = mybir.AluOpType
 ACT = mybir.ActivationFunctionType
 
+PA = {-5:0,-4:1,-3:1,-2:1,-1:1}
+PB = {-5:3,-4:3,-3:2,-2:0,-1:0}
+PS = [(1,1),(1,1),(1,1),(0,0)]
 GROUPS = 4
 RHO = 10000.0 ** (-1.0 / HALF)
 TWO_PI = 2.0 * math.pi
@@ -42,10 +45,10 @@ def tile_multiheadlatentattention_pa_t_w4_kernel(
         xin = ctx.enter_context(tc.tile_pool(name="xin", bufs=8))
         work = ctx.enter_context(tc.tile_pool(name="work", bufs=3))
         tabs = ctx.enter_context(tc.tile_pool(name="tabs", bufs=3))
-        outs = ctx.enter_context(tc.tile_pool(name="outs", bufs=4))
+        outs = ctx.enter_context(tc.tile_pool(name="outs", bufs=3))
         psum = ctx.enter_context(tc.psum_pool(name="psum", bufs=1))
 
-        scale_row = keep.tile([P, 2, D], F32, name="scale_row")
+        scale_row = keep.tile([P, 4, D], F32, name="scale_row")
         x_tiles = {}
 
         def load_x(g, b):
@@ -68,11 +71,11 @@ def tile_multiheadlatentattention_pa_t_w4_kernel(
         down_raw = keep.tile([P, 2 * D], U8, name="down_raw", align_bytes=64)
         up_codes = keep.tile([P, 2 * D], U8, name="up_codes", align_bytes=64)
         rope_codes = keep.tile([P, 2 * D], U8, name="rope_codes", align_bytes=64)
-        load_x(0, 0)
-        load_x(0, 1)
         nc.sync.dma_start(out=scale_row[:, 0, :], in_=x_scale.rearrange("a o k -> (a o k)").partition_broadcast(P))
+        load_x(0, 0)
         nc.sync.dma_start(out=down_raw[:], in_=down_words[0])
         load_scales(0, down_scales)
+        load_x(0, 1)
         nc.sync.dma_start(out=rope_codes[:], in_=rope_words[0])
         load_scales(2, rope_scales)
         nc.sync.dma_start(out=up_codes[:], in_=up_words[0])
@@ -111,9 +114,9 @@ def tile_multiheadlatentattention_pa_t_w4_kernel(
         turns = keep.tile([P, 4 * GROUPS, HALF], F32, name="turns")
         whole = keep.tile([P, 4 * GROUPS, 192], I32, name="whole")
 
-        def raw_angles(eng, unit):
-            j0 = reduced_columns(unit // 2)
-            for c in (2 * unit, 2 * unit + 1):
+        def raw_angles(eng, first, last):
+            for c in range(first, last):
+                j0 = reduced_columns(c // 4)
                 eng.tensor_scalar(
                     out=whole[:, c, 0:j0], in0=freq[:, 0:j0], scalar1=pos[:, c : c + 1], scalar2=0.0,
                     op0=ALU.mult, op1=ALU.add,
@@ -124,83 +127,98 @@ def tile_multiheadlatentattention_pa_t_w4_kernel(
                 )
 
         def reduce_angles(first, last):
-            j0 = reduced_columns(first // 2)
-            part = turns[:, 2 * first : 2 * last, 0:j0]
-            nc.vector.tensor_tensor(out=part, in0=part, in1=whole[:, 2 * first : 2 * last, 0:j0], op=ALU.subtract)
+            j0 = reduced_columns(first // 4)
+            part = turns[:, first:last, 0:j0]
+            nc.vector.tensor_tensor(out=part, in0=part, in1=whole[:, first:last, 0:j0], op=ALU.subtract)
 
         tables = {}
 
-        def table_steps(unit):
-            j0 = reduced_columns(unit // 2)
-            sin_t = tabs.tile([P, 2, HALF], F32, name="sin_t")
-            mix_t = tabs.tile([P, 2, D], F32, name="mix_t")
-            a1 = tabs.tile([P, 2, 192], F32, name="a1")
-            a2 = tabs.tile([P, 2, 192], F32, name="a2")
-            tables[unit] = (sin_t, mix_t)
-            tu = turns[:, 2 * unit : 2 * unit + 2, :]
-            low, high = tu[:, :, 0:j0], tu[:, :, j0:HALF]
+        def table_steps(first, last):
+            g = first // 4
+            j0 = reduced_columns(g)
+            if first % 4 == 0:
+                sin_t = tabs.tile([P, 4, HALF], F32, name="sin_t")
+                mix_t = tabs.tile([P, 4, 2, HALF], F32, name="mix_t")
+                bent = tabs.tile([P, 4, 2, 192], F32, name="bent")
+                tables[g] = (sin_t, mix_t, bent)
+            sin_t, mix_t, bent = tables[g]
+            own = slice(first - 4 * g, last - 4 * g)
+            low, high = turns[:, first:last, 0:j0], turns[:, first:last, j0:HALF]
 
             def act(o, i, f, bias, scale):
                 return lambda: nc.scalar.activation(out=o, in_=i, func=f, bias=bias, scale=scale)
 
             q = math.pi / 4
             return [
-                act(a1[:, :, 0:j0], low, ACT.Abs, -q, TWO_PI),
-                act(a2[:, :, 0:j0], low, ACT.Abs, q, TWO_PI),
-                act(mix_t[:, :, j0:HALF], high, ACT.Sin, 3 * q, -TWO_PI),
-                act(mix_t[:, :, 0:j0], a1[:, :, 0:j0], ACT.Sin, 2 * q, -1.0),
-                act(mix_t[:, :, HALF + j0 : D], high, ACT.Sin, q, -TWO_PI),
-                act(mix_t[:, :, HALF : HALF + j0], a2[:, :, 0:j0], ACT.Sin, 2 * q, -1.0),
-                act(sin_t[:], tu, ACT.Sin, 0.0, TWO_PI),
+                act(bent[:, own, 0, 0:j0], low, ACT.Abs, -q, TWO_PI),
+                act(bent[:, own, 1, 0:j0], low, ACT.Abs, q, TWO_PI),
+                act(mix_t[:, own, 0, j0:HALF], high, ACT.Sin, 3 * q, -TWO_PI),
+                act(mix_t[:, own, 1, j0:HALF], high, ACT.Sin, q, -TWO_PI),
+                act(mix_t[:, own, :, 0:j0], bent[:, own, :, 0:j0], ACT.Sin, 2 * q, -1.0),
+                act(sin_t[:, own, :], turns[:, first:last, :], ACT.Sin, 0.0, TWO_PI),
             ]
 
         down_codes = keep.tile([P, 4, 2 * P], U8, name="down_codes", align_bytes=64)
         down_plane = keep.tile([P, 4, P], U8, name="down_plane", align_bytes=64)
 
-        chunks = [(g, b, h) for g in range(GROUPS) for h in range(2) for b in range(B)]
+        chunks = [(g, b, h) for g in range(GROUPS) for b in range(B) for h in range(2)]
+        n = len(chunks)
         xw, xg, xq, lg, lq = {}, {}, {}, {}, {}
+        stages, mixes, sines, u_banks = {}, {}, {}, {}
 
-        def widen(c):
-            g, b, h = chunks[c]
-            xw[c] = work.tile([P, 2 * D], BF16, name="xw", align_bytes=64)
+        def cols(i):
+            return slice(P * i, P * (i + 1))
+
+        def widen(first, last):
+            g, b, h = chunks[first]
+            if h == 0:
+                xw[first // 2] = work.tile([P, 2, 2 * D], BF16, name="xw", align_bytes=64)
             nc.vector.tensor_tensor(
-                out=xw[c][:],
-                in0=x_tiles[(g, b)][:, 2 * D * h : 2 * D * (h + 1)].bitcast(FP8),
-                in1=scale2,
+                out=xw[first // 2][:, h : h + last - first, :].rearrange("p c k -> p (c k)"),
+                in0=x_tiles[(g, b)][:, 2 * D * h : 2 * D * (h + last - first)].bitcast(FP8),
+                in1=scale_row[:].rearrange("p i k -> p (i k)")[:, 0 : 2 * D * (last - first)],
                 op=ALU.mult,
             )
 
         def turn(c):
-            words = xw[c][:].bitcast(F32)
+            words = xw[c // 2][:, c % 2, :].bitcast(F32)
             bank = psum.tile([P, 2, 2, P], F32, name="xt_bank")
             for i in range(2):
                 for u in range(2):
                     nc.tensor.transpose(bank[:, i, u, :], words[:, 256 * i + u : 256 * (i + 1) : 2], ident[:])
-            xg[c] = work.tile([P, 4 * 256], BF16, name="xg", align_bytes=64)
+            if c % 2 == 0:
+                xg[c // 2] = work.tile([P, 2, 4 * 256], BF16, name="xg", align_bytes=64)
             nc.scalar.copy(
-                out=xg[c][:].bitcast(F32).rearrange("p (i r u) -> p i r u", i=2, u=2),
+                out=xg[c // 2][:, c % 2, :].bitcast(F32).rearrange("p (i r u) -> p i r u", i=2, u=2),
                 in_=bank[:].rearrange("p i u r -> p i r u"),
             )
 
-        def quant(src, tag):
-            codes = work.tile([P, 256], U32, name=tag + "_codes", align_bytes=64)
-            plane = work.tile([P, 256], U8, name=tag + "_plane", align_bytes=64)
-            nc.vector.quantize_mx(out=codes[:].bitcast(FP8X4), scales=plane[:], in_=src[:])
-            return codes, plane
+        def quant_x(first, last):
+            h = first % 2
+            if h == 0:
+                codes = work.tile([P, 2, 256], U32, name="x_codes", align_bytes=64)
+                plane = work.tile([P, 2, 256], U8, name="x_plane", align_bytes=64)
+                xq[first // 2] = (codes, plane)
+            codes, plane = xq[first // 2]
+            own = slice(h, h + last - first)
+            nc.vector.quantize_mx(
+                out=codes[:, own, :].rearrange("p c n -> p (c n)").bitcast(FP8X4),
+                scales=plane[:, own, :].rearrange("p c n -> p (c n)"),
+                in_=xg[first // 2][:, own, :].rearrange("p c n -> p (c n)"),
+            )
 
         def latent(c):
-            codes, plane = xq[c]
+            codes, plane = xq[c // 2]
             lg[c] = work.tile([P, 4 * 256], BF16, name="lg", align_bytes=64)
             for i in range(2):
-                cols = slice(P * i, P * (i + 1))
                 bank = psum.tile([P, 4, P], F32, name="lat_bank%d" % i)
                 for t in range(4):
                     nc.tensor.matmul_mx(
                         out=bank[:, t, :],
                         lhsT=down_codes[:, t, :].bitcast(FP4X4),
                         lhsT_scale=down_plane[:, t, :],
-                        rhs=codes[:, cols].bitcast(FP8X4),
-                        rhs_scale=plane[:, cols],
+                        rhs=codes[:, c % 2, cols(i)].bitcast(FP8X4),
+                        rhs_scale=plane[:, c % 2, cols(i)],
                         start=True,
                         stop=True,
                     )
@@ -209,22 +227,31 @@ def tile_multiheadlatentattention_pa_t_w4_kernel(
                     in_=bank[:].rearrange("p t n -> p n t"),
                 )
 
-        stages, mixes, sines, u_banks, q_banks = {}, {}, {}, {}, {}
+        def quant_latent(c):
+            codes = work.tile([P, 256], U32, name="l_codes", align_bytes=64)
+            plane = work.tile([P, 256], U8, name="l_plane", align_bytes=64)
+            nc.vector.quantize_mx(out=codes[:].bitcast(FP8X4), scales=plane[:], in_=lg[c][:])
+            lq[c] = (codes, plane)
+
+        def pair_of(c):
+            return (c + 1) // 2
 
         def project(c):
             codes, plane = lq[c]
-            stages[c] = outs.tile([P, 2, H, 256], F32, name="stage")
-            mixes[c] = work.tile([P, 2, D], F32, name="mixed")
-            sines[c] = work.tile([P, 2, HALF], F32, name="sined")
-            u_bank = psum.tile([P, 2, HALF], F32, name="u_bank")
             g, b, h = chunks[c]
+            p = pair_of(c)
+            if p not in stages:
+                stages[p] = outs.tile([P, 2, 2, H, 256], F32, name="stage")
+                mixes[p] = work.tile([P, 2, 2, D], F32, name="mixed")
+                sines[p] = work.tile([P, 2, 2, HALF], F32, name="sined")
+            e = (c + 1) % 2
+            u_banks[c] = psum.tile([P, 2, HALF], F32, name="u_bank")
 
             def mm(i, o, words, pl, a, n, start, stop):
-                cols = slice(P * i, P * (i + 1))
                 nc.tensor.matmul_mx(
                     out=o,
-                    lhsT=codes[:, cols].bitcast(FP8X4),
-                    lhsT_scale=plane[:, cols],
+                    lhsT=codes[:, cols(i)].bitcast(FP8X4),
+                    lhsT_scale=plane[:, cols(i)],
                     rhs=words[:, 2 * a : 2 * (a + n)].bitcast(FP4X4),
                     rhs_scale=planes[:, pl, a : a + n],
                     start=start,
@@ -235,45 +262,39 @@ def tile_multiheadlatentattention_pa_t_w4_kernel(
                 r_bank = psum.tile([P, D], F32, name="r_bank%d" % i)
                 mm(i, r_bank[:], rope_codes, 2, 0, D, True, True)
                 nc.vector.scalar_tensor_tensor(
-                    out=mixes[c][:, i, :], in0=r_bank[:], scalar=math.sqrt(2.0), in1=tables[2 * g + h][1][:, i, :],
+                    out=mixes[p][:, e, i, :], in0=r_bank[:], scalar=math.sqrt(2.0),
+                    in1=tables[g][1][:, 2 * h + i, :, :].rearrange("p s c -> p (s c)"),
                     op0=ALU.mult, op1=ALU.mult,
                 )
             for i in range(2):
                 for half in range(2):
-                    mm(i, u_bank[:, i, P * half : P * (half + 1)], rope_codes, 2, P * half, P, True, False)
-                    mm(i, u_bank[:, i, P * half : P * (half + 1)], rope_codes, 2, HALF + P * half, P, False, True)
-            u_banks[c] = u_bank
+                    o = u_banks[c][:, i, P * half : P * (half + 1)]
+                    mm(i, o, rope_codes, 2, P * half, P, True, False)
+                    mm(i, o, rope_codes, 2, HALF + P * half, P, False, True)
+            nc.vector.tensor_tensor(
+                out=sines[p][:, e, :, :], in0=u_banks[c][:], in1=tables[g][0][:, 2 * h : 2 * h + 2, :], op=ALU.mult
+            )
             for i in range(2):
                 q_bank = psum.tile([P, D], F32, name="q_bank%d" % i)
                 mm(i, q_bank[:], up_codes, 1, 0, D, True, True)
-                nc.scalar.copy(
-                    out=stages[c][:, i, :, 0:P], in_=q_bank[:].rearrange("p (h c) -> p h c", h=H)
-                )
+                nc.scalar.copy(out=stages[p][:, e, i, :, 0:P], in_=q_bank[:].rearrange("p (h c) -> p h c", h=H))
 
-        def sine_part(c):
-            g, b, h = chunks[c]
-            nc.vector.tensor_tensor(
-                out=sines[c][:], in0=u_banks[c][:], in1=tables[2 * g + h][0][:], op=ALU.mult
+        def combine(eng, first_chunk, last_chunk, head, op):
+            p = pair_of(first_chunk)
+            e0 = (first_chunk + 1) % 2
+            own = slice(e0, e0 + last_chunk - first_chunk)
+            m = 2 * (last_chunk - first_chunk)
+            eng.tensor_tensor(
+                out=stages[p][:, own].rearrange("p e i h c -> p (e i) h c")[:, :, head : head + 2, P:256],
+                in0=mixes[p][:, own].rearrange("p e i (h c) -> p (e i) h c", h=H)[:, :, head : head + 2, :],
+                in1=sines[p][:, own].rearrange("p e i (h c) -> p (e i) h c", h=2),
+                op=op,
             )
 
-        def first_half(c):
+        def store(c):
             g, b, h = chunks[c]
-            nc.vector.tensor_tensor(
-                out=stages[c][:, :, 0:2, P:256],
-                in0=mixes[c][:, :, 0:HALF].rearrange("p i (h c) -> p i h c", h=2),
-                in1=sines[c][:].rearrange("p i (h c) -> p i h c", h=2),
-                op=ALU.subtract,
-            )
-            nc.vector.tensor_tensor(
-                out=stages[c][:, :, 2:4, P:256],
-                in0=mixes[c][:, :, HALF:D].rearrange("p i (h c) -> p i h c", h=2),
-                in1=sines[c][:].rearrange("p i (h c) -> p i h c", h=2),
-                op=ALU.add,
-            )
-            nc.sync.dma_start(
-                out=out[b, 512 * g : 512 * g + 512, :, :].rearrange("(p i) h c -> p i h c", i=4)[:, 2 * h : 2 * h + 2],
-                in_=stages[c][:],
-            )
+            rows = out[b, 512 * g : 512 * g + 512, :, :].rearrange("(p i) h c -> p i h c", i=4)
+            nc.sync.dma_start(out=rows[:, 2 * h : 2 * h + 2], in_=stages[pair_of(c)][:, (c + 1) % 2])
 
         def prepare_down():
             nc.vector.tensor_copy(
@@ -284,45 +305,62 @@ def tile_multiheadlatentattention_pa_t_w4_kernel(
                 out=down_plane[:], in_=planes[:, 0, :].rearrange("p (m t) -> p t m", t=4)
             )
 
-        n = len(chunks)
-        units = 2 * GROUPS
-        queue = []
+        pieces = []
+
+        def table_piece(count):
+            for i in range(count):
+                if pieces:
+                    pieces.pop(0)()
+
         with tc.manual_schedule():
-            raw_angles(nc.vector, 0)
-            for unit in range(1, units):
-                raw_angles(nc.gpsimd, unit)
-            reduce_angles(0, 1)
+            raw_angles(nc.vector, 0, 2)
+            reduce_angles(0, 2)
+            raw_angles(nc.gpsimd, 2, 4)
             nc.scalar.copy(out=scale_row[:, 1, :], in_=scale_row[:, 0, :])
-            queued = 0
-            for k in range(-5, n + 1):
-                if 0 <= k < n:
+            nc.gpsimd.tensor_scalar(
+                out=scale_row[:, 2:4, :], in0=scale_row[:, 0:2, :], scalar1=1.0, scalar2=0.0,
+                op0=ALU.mult, op1=ALU.add,
+            )
+            raw_angles(nc.gpsimd, 4, 16)
+            for k in range(-5, n):
+                if 0 <= k:
                     project(k)
-                if 0 <= k + 1 < n:
-                    lq[k + 1] = quant(lg[k + 1], "l")
-                if k == -3:
-                    prepare_down()
-                    reduce_angles(1, 2)
-                if k == -2:
-                    reduce_angles(2, 4)
-                if k == -1:
-                    reduce_angles(4, 6)
-                    reduce_angles(6, 8)
-                if 0 <= k + 3 < n:
-                    xq[k + 3] = quant(xg[k + 3], "x")
-                if 0 <= k + 5 < n:
-                    widen(k + 5)
-                if 0 <= k - 1 < n:
-                    first_half(k - 1)
-                if 0 <= k < n:
-                    sine_part(k)
+                    combine(nc.gpsimd, k, k + 1, 2, ALU.add)
+                table_piece(PA.get(k, PS[k % 4][0]))
                 if 0 <= k + 2 < n:
                     latent(k + 2)
-                if 0 <= k + 4 < n:
-                    turn(k + 4)
-                take = 2 if k < 0 else 4
-                for i in range(take):
-                    if not queue and queued < units and 2 * queued <= k + 5:
-                        queue = table_steps(queued)
-                        queued += 1
-                    if queue:
-                        queue.pop(0)()
+                if 0 <= k + 1 < n:
+                    quant_latent(k + 1)
+                if k == -5:
+                    widen(0, 1)
+                    prepare_down()
+                    pieces.extend(table_steps(0, 2))
+                if k == -4:
+                    widen(1, 2)
+                    reduce_angles(2, 4)
+                    pieces.extend(table_steps(2, 4))
+                if 0 <= k + 5 < n:
+                    turn(k + 5)
+                if k in (-4, -3):
+                    quant_x(k + 4, k + 5)
+                if k >= -4 and k % 2 == 0 and k + 6 < n:
+                    widen(k + 6, k + 8)
+                if k >= -1 and k % 2 == 1 and k + 3 < n:
+                    quant_x(k + 3, k + 5)
+                if -3 <= k < 0:
+                    reduce_angles(4 * k + 16, 4 * k + 20)
+                if k == 1:
+                    combine(nc.vector, 0, 1, 0, ALU.subtract)
+                    store(0)
+                if 3 <= k <= n - 7 and k % 2 == 1:
+                    combine(nc.vector, k - 2, k, 0, ALU.subtract)
+                    store(k - 2)
+                    store(k - 1)
+                if k >= n - 6:
+                    combine(nc.vector, k - 1, k, 0, ALU.subtract)
+                    store(k - 1)
+                if k >= -1 and k % 4 == 3 and (k + 1) // 4 + 1 < GROUPS:
+                    pieces.extend(table_steps(k + 5, k + 9))
+                table_piece(PB.get(k, PS[k % 4][1]))
+            combine(nc.vector, n - 1, n, 0, ALU.subtract)
+            store(n - 1)

@@ -20,12 +20,11 @@ FP4X4 = mybir.dt.float4_e2m1fn_x4
 ALU = mybir.AluOpType
 ACT = mybir.ActivationFunctionType
 
-PA = {-5:0,-4:1,-3:1,-2:1,-1:1}
-PB = {-5:3,-4:3,-3:2,-2:0,-1:0}
-PS = [(1,1),(1,1),(1,1),(0,0)]
 GROUPS = 4
 RHO = 10000.0 ** (-1.0 / HALF)
 TWO_PI = 2.0 * math.pi
+PS = [(1,1),(1,1),(1,1),(0,0)]
+VQ = [(), (), (1,), ()]
 
 
 def reduced_columns(group):
@@ -45,10 +44,9 @@ def tile_multiheadlatentattention_pa_t_w4_kernel(
         xin = ctx.enter_context(tc.tile_pool(name="xin", bufs=8))
         work = ctx.enter_context(tc.tile_pool(name="work", bufs=3))
         tabs = ctx.enter_context(tc.tile_pool(name="tabs", bufs=3))
-        outs = ctx.enter_context(tc.tile_pool(name="outs", bufs=3))
+        outs = ctx.enter_context(tc.tile_pool(name="outs", bufs=5))
         psum = ctx.enter_context(tc.psum_pool(name="psum", bufs=1))
 
-        scale_row = keep.tile([P, 4, D], F32, name="scale_row")
         x_tiles = {}
 
         def load_x(g, b):
@@ -68,11 +66,14 @@ def tile_multiheadlatentattention_pa_t_w4_kernel(
                     in_=scales[0, 4 * q : 4 * q + 4, :].bitcast(I32),
                 )
 
+        x_factor = keep.tile([P, 1, 2, 2], F32, name="x_factor")
         down_raw = keep.tile([P, 2 * D], U8, name="down_raw", align_bytes=64)
         up_codes = keep.tile([P, 2 * D], U8, name="up_codes", align_bytes=64)
         rope_codes = keep.tile([P, 2 * D], U8, name="rope_codes", align_bytes=64)
-        nc.sync.dma_start(out=scale_row[:, 0, :], in_=x_scale.rearrange("a o k -> (a o k)").partition_broadcast(P))
         load_x(0, 0)
+        nc.sync.dma_start(
+            out=x_factor[:].rearrange("p o u e -> p (o u e)"), in_=x_scale.rearrange("a o (p t) -> p (a o t)", t=4)
+        )
         nc.sync.dma_start(out=down_raw[:], in_=down_words[0])
         load_scales(0, down_scales)
         load_x(0, 1)
@@ -80,10 +81,9 @@ def tile_multiheadlatentattention_pa_t_w4_kernel(
         load_scales(2, rope_scales)
         nc.sync.dma_start(out=up_codes[:], in_=up_words[0])
         load_scales(1, up_scales)
-        for g in range(GROUPS):
+        for g in range(1, GROUPS):
             for b in range(B):
-                if g > 0:
-                    load_x(g, b)
+                load_x(g, b)
 
         dummy = keep.tile([P, 1], F32, name="dummy")
         nc.vector.memset(dummy[:], 0.0)
@@ -109,7 +109,6 @@ def tile_multiheadlatentattention_pa_t_w4_kernel(
             w *= 2
         ident = keep.tile([P, P], F32, name="ident")
         make_identity(nc, ident[:])
-        scale2 = scale_row[:].rearrange("p i k -> p (i k)")
 
         turns = keep.tile([P, 4 * GROUPS, HALF], F32, name="turns")
         whole = keep.tile([P, 4 * GROUPS, 192], I32, name="whole")
@@ -169,28 +168,28 @@ def tile_multiheadlatentattention_pa_t_w4_kernel(
         def cols(i):
             return slice(P * i, P * (i + 1))
 
-        def widen(first, last):
+        def widen(copy, first, last):
             g, b, h = chunks[first]
             if h == 0:
                 xw[first // 2] = work.tile([P, 2, 2 * D], BF16, name="xw", align_bytes=64)
-            nc.vector.tensor_tensor(
+            copy(
                 out=xw[first // 2][:, h : h + last - first, :].rearrange("p c k -> p (c k)"),
-                in0=x_tiles[(g, b)][:, 2 * D * h : 2 * D * (h + last - first)].bitcast(FP8),
-                in1=scale_row[:].rearrange("p i k -> p (i k)")[:, 0 : 2 * D * (last - first)],
-                op=ALU.mult,
+                in_=x_tiles[(g, b)][:, 2 * D * h : 2 * D * (h + last - first)].bitcast(FP8),
             )
 
         def turn(c):
             words = xw[c // 2][:, c % 2, :].bitcast(F32)
-            bank = psum.tile([P, 2, 2, P], F32, name="xt_bank")
+            bank = psum.tile([P, 2, 2 * P], F32, name="u_bank" if c in (1, 3) else "xt_bank")
             for i in range(2):
                 for u in range(2):
-                    nc.tensor.transpose(bank[:, i, u, :], words[:, 256 * i + u : 256 * (i + 1) : 2], ident[:])
+                    nc.tensor.transpose(bank[:, u, cols(i)], words[:, 256 * i + u : 256 * (i + 1) : 2], ident[:])
             if c % 2 == 0:
                 xg[c // 2] = work.tile([P, 2, 4 * 256], BF16, name="xg", align_bytes=64)
-            nc.scalar.copy(
-                out=xg[c // 2][:, c % 2, :].bitcast(F32).rearrange("p (i r u) -> p i r u", i=2, u=2),
-                in_=bank[:].rearrange("p i u r -> p i r u"),
+            nc.vector.tensor_tensor(
+                out=xg[c // 2][:, c % 2, :].rearrange("p (r u e) -> p r u e", u=2, e=2),
+                in0=bank[:].bitcast(BF16).rearrange("p u (r e) -> p r u e", e=2),
+                in1=x_factor[:].to_broadcast([P, 256, 2, 2]),
+                op=ALU.mult,
             )
 
         def quant_x(first, last):
@@ -233,68 +232,82 @@ def tile_multiheadlatentattention_pa_t_w4_kernel(
             nc.vector.quantize_mx(out=codes[:].bitcast(FP8X4), scales=plane[:], in_=lg[c][:])
             lq[c] = (codes, plane)
 
-        def pair_of(c):
-            return (c + 1) // 2
-
-        def project(c):
+        def mm(c, i, o, words, pl, a, count, start, stop):
             codes, plane = lq[c]
+            nc.tensor.matmul_mx(
+                out=o,
+                lhsT=codes[:, cols(i)].bitcast(FP8X4),
+                lhsT_scale=plane[:, cols(i)],
+                rhs=words[:, 2 * a : 2 * (a + count)].bitcast(FP4X4),
+                rhs_scale=planes[:, pl, a : a + count],
+                start=start,
+                stop=stop,
+            )
+
+        def project_rope(c):
             g, b, h = chunks[c]
-            p = pair_of(c)
-            if p not in stages:
-                stages[p] = outs.tile([P, 2, 2, H, 256], F32, name="stage")
-                mixes[p] = work.tile([P, 2, 2, D], F32, name="mixed")
-                sines[p] = work.tile([P, 2, 2, HALF], F32, name="sined")
-            e = (c + 1) % 2
-            u_banks[c] = psum.tile([P, 2, HALF], F32, name="u_bank")
-
-            def mm(i, o, words, pl, a, n, start, stop):
-                nc.tensor.matmul_mx(
-                    out=o,
-                    lhsT=codes[:, cols(i)].bitcast(FP8X4),
-                    lhsT_scale=plane[:, cols(i)],
-                    rhs=words[:, 2 * a : 2 * (a + n)].bitcast(FP4X4),
-                    rhs_scale=planes[:, pl, a : a + n],
-                    start=start,
-                    stop=stop,
-                )
-
+            stages[c] = outs.tile([P, 2, H, 256], F32, name="stage")
+            mixes[c] = work.tile([P, 2, D], F32, name="mixed")
+            sines[c] = work.tile([P, 2, HALF], F32, name="sined")
             for i in range(2):
                 r_bank = psum.tile([P, D], F32, name="r_bank%d" % i)
-                mm(i, r_bank[:], rope_codes, 2, 0, D, True, True)
+                mm(c, i, r_bank[:], rope_codes, 2, 0, D, True, True)
                 nc.vector.scalar_tensor_tensor(
-                    out=mixes[p][:, e, i, :], in0=r_bank[:], scalar=math.sqrt(2.0),
+                    out=mixes[c][:, i, :], in0=r_bank[:], scalar=math.sqrt(2.0),
                     in1=tables[g][1][:, 2 * h + i, :, :].rearrange("p s c -> p (s c)"),
                     op0=ALU.mult, op1=ALU.mult,
                 )
+
+        def project_up(c):
+            for i in range(2):
+                q_bank = psum.tile([P, D], F32, name="q_bank%d" % i)
+                mm(c, i, q_bank[:], up_codes, 1, 0, D, True, True)
+                copy = nc.vector.tensor_copy if i in VQ[c % 4] else nc.scalar.copy
+                copy(out=stages[c][:, i, :, 0:P], in_=q_bank[:].rearrange("p (h c) -> p h c", h=H))
+
+        def project_sum(c):
+            u_banks[c] = psum.tile([P, 2, HALF], F32, name="u_bank")
             for i in range(2):
                 for half in range(2):
                     o = u_banks[c][:, i, P * half : P * (half + 1)]
-                    mm(i, o, rope_codes, 2, P * half, P, True, False)
-                    mm(i, o, rope_codes, 2, HALF + P * half, P, False, True)
-            nc.vector.tensor_tensor(
-                out=sines[p][:, e, :, :], in0=u_banks[c][:], in1=tables[g][0][:, 2 * h : 2 * h + 2, :], op=ALU.mult
-            )
-            for i in range(2):
-                q_bank = psum.tile([P, D], F32, name="q_bank%d" % i)
-                mm(i, q_bank[:], up_codes, 1, 0, D, True, True)
-                nc.scalar.copy(out=stages[p][:, e, i, :, 0:P], in_=q_bank[:].rearrange("p (h c) -> p h c", h=H))
+                    mm(c, i, o, rope_codes, 2, P * half, P, True, False)
+                    mm(c, i, o, rope_codes, 2, HALF + P * half, P, False, True)
 
-        def combine(eng, first_chunk, last_chunk, head, op):
-            p = pair_of(first_chunk)
-            e0 = (first_chunk + 1) % 2
-            own = slice(e0, e0 + last_chunk - first_chunk)
-            m = 2 * (last_chunk - first_chunk)
+        def sine_part(c):
+            g, b, h = chunks[c]
+            nc.vector.tensor_tensor(
+                out=sines[c][:], in0=u_banks[c][:], in1=tables[g][0][:, 2 * h : 2 * h + 2, :], op=ALU.mult
+            )
+
+        def combine(eng, c, head, op):
             eng.tensor_tensor(
-                out=stages[p][:, own].rearrange("p e i h c -> p (e i) h c")[:, :, head : head + 2, P:256],
-                in0=mixes[p][:, own].rearrange("p e i (h c) -> p (e i) h c", h=H)[:, :, head : head + 2, :],
-                in1=sines[p][:, own].rearrange("p e i (h c) -> p (e i) h c", h=2),
+                out=stages[c][:, :, head : head + 2, P:256],
+                in0=mixes[c][:].rearrange("p i (h c) -> p i h c", h=H)[:, :, head : head + 2, :],
+                in1=sines[c][:].rearrange("p i (h c) -> p i h c", h=2),
                 op=op,
             )
 
         def store(c):
             g, b, h = chunks[c]
             rows = out[b, 512 * g : 512 * g + 512, :, :].rearrange("(p i) h c -> p i h c", i=4)
-            nc.sync.dma_start(out=rows[:, 2 * h : 2 * h + 2], in_=stages[pair_of(c)][:, (c + 1) % 2])
+            nc.sync.dma_start(out=rows[:, 2 * h : 2 * h + 2], in_=stages[c][:])
+
+        def last_chunk(c):
+            g, b, h = chunks[c]
+            rows = out[b, 512 * g : 512 * g + 512, :, :].rearrange("(p i) h c -> p i h c", i=4)
+            for i in range(2):
+                nc.vector.tensor_tensor(
+                    out=sines[c][:, i, :], in0=u_banks[c][:, i, :], in1=tables[g][0][:, 2 * h + i, :], op=ALU.mult
+                )
+            for i in range(2):
+                for eng, head, op in ((nc.vector, 0, ALU.subtract), (nc.gpsimd, 2, ALU.add)):
+                    eng.tensor_tensor(
+                        out=stages[c][:, i, head : head + 2, P:256],
+                        in0=mixes[c][:, i, :].rearrange("p (h c) -> p h c", h=H)[:, head : head + 2, :],
+                        in1=sines[c][:, i, :].rearrange("p (h c) -> p h c", h=2),
+                        op=op,
+                    )
+                nc.sync.dma_start(out=rows[:, 2 * h + i], in_=stages[c][:, i])
 
         def prepare_down():
             nc.vector.tensor_copy(
@@ -314,53 +327,57 @@ def tile_multiheadlatentattention_pa_t_w4_kernel(
 
         with tc.manual_schedule():
             raw_angles(nc.vector, 0, 2)
+            widen(nc.vector.tensor_copy, 0, 1)
             reduce_angles(0, 2)
-            raw_angles(nc.gpsimd, 2, 4)
-            nc.scalar.copy(out=scale_row[:, 1, :], in_=scale_row[:, 0, :])
-            nc.gpsimd.tensor_scalar(
-                out=scale_row[:, 2:4, :], in0=scale_row[:, 0:2, :], scalar1=1.0, scalar2=0.0,
-                op0=ALU.mult, op1=ALU.add,
-            )
-            raw_angles(nc.gpsimd, 4, 16)
-            for k in range(-5, n):
-                if 0 <= k:
-                    project(k)
-                    combine(nc.gpsimd, k, k + 1, 2, ALU.add)
-                table_piece(PA.get(k, PS[k % 4][0]))
-                if 0 <= k + 2 < n:
+            raw_angles(nc.gpsimd, 2, 16)
+            pieces.extend(table_steps(0, 2))
+            widen(nc.vector.tensor_copy, 1, 2)
+            table_piece(2)
+            widen(nc.scalar.copy, 2, 4)
+            prepare_down()
+            turn(0)
+            reduce_angles(2, 4)
+            table_piece(4)
+            pieces.extend(table_steps(2, 4))
+            quant_x(0, 1)
+            turn(1)
+            latent(0)
+            table_piece(2)
+            quant_x(1, 2)
+            turn(2)
+            widen(nc.scalar.copy, 4, 6)
+            latent(1)
+            table_piece(2)
+            quant_latent(0)
+            turn(3)
+            quant_x(2, 4)
+            reduce_angles(4, 8)
+            table_piece(2)
+            pieces.extend(table_steps(4, 8))
+            for k in range(n):
+                project_rope(k)
+                if k + 4 < n:
+                    turn(k + 4)
+                project_up(k)
+                table_piece(PS[k % 4][0])
+                project_sum(k)
+                if k + 2 < n:
                     latent(k + 2)
-                if 0 <= k + 1 < n:
+                if k + 1 < n:
                     quant_latent(k + 1)
-                if k == -5:
-                    widen(0, 1)
-                    prepare_down()
-                    pieces.extend(table_steps(0, 2))
-                if k == -4:
-                    widen(1, 2)
-                    reduce_angles(2, 4)
-                    pieces.extend(table_steps(2, 4))
-                if 0 <= k + 5 < n:
-                    turn(k + 5)
-                if k in (-4, -3):
-                    quant_x(k + 4, k + 5)
-                if k >= -4 and k % 2 == 0 and k + 6 < n:
-                    widen(k + 6, k + 8)
-                if k >= -1 and k % 2 == 1 and k + 3 < n:
+                if k % 2 == 1 and k + 3 < n:
                     quant_x(k + 3, k + 5)
-                if -3 <= k < 0:
-                    reduce_angles(4 * k + 16, 4 * k + 20)
-                if k == 1:
-                    combine(nc.vector, 0, 1, 0, ALU.subtract)
-                    store(0)
-                if 3 <= k <= n - 7 and k % 2 == 1:
-                    combine(nc.vector, k - 2, k, 0, ALU.subtract)
-                    store(k - 2)
-                    store(k - 1)
-                if k >= n - 6:
-                    combine(nc.vector, k - 1, k, 0, ALU.subtract)
-                    store(k - 1)
-                if k >= -1 and k % 4 == 3 and (k + 1) // 4 + 1 < GROUPS:
+                if k in (1, 5):
+                    reduce_angles(k + 7, k + 11)
+                if k == n - 1:
+                    last_chunk(k)
+                else:
+                    sine_part(k)
+                    combine(nc.vector if k >= n - 2 else nc.gpsimd, k, 0, ALU.subtract)
+                    combine(nc.gpsimd, k, 2, ALU.add)
+                    store(k)
+                if k % 2 == 0 and k + 6 < n:
+                    widen(nc.scalar.copy, k + 6, k + 8)
+                if k % 4 == 3 and (k + 1) // 4 + 1 < GROUPS:
                     pieces.extend(table_steps(k + 5, k + 9))
-                table_piece(PB.get(k, PS[k % 4][1]))
-            combine(nc.vector, n - 1, n, 0, ALU.subtract)
-            store(n - 1)
+                table_piece(PS[k % 4][1])

@@ -4,11 +4,6 @@ from contextlib import ExitStack
 import concourse.mybir as mybir
 from concourse.masks import make_identity
 
-B, S, D, H = 2, 2048, 512, 4
-P = 128
-HALF = D // 2
-FLOPS = 3 * 2 * B * S * D * D
-
 F32 = mybir.dt.float32
 BF16 = mybir.dt.bfloat16
 I32 = mybir.dt.int32
@@ -20,19 +15,42 @@ FP4X4 = mybir.dt.float4_e2m1fn_x4
 ALU = mybir.AluOpType
 ACT = mybir.ActivationFunctionType
 
-GROUPS = 4
-RHO = 10000.0 ** (-1.0 / HALF)
+BATCH, SEQ, WIDTH, HEADS = 2, 2048, 512, 4
+FLOPS = 3 * 2 * BATCH * SEQ * WIDTH * WIDTH
+
+P = 128
+HALF = WIDTH // 2
+GROUP = 512
+GROUPS = SEQ // GROUP
+TILES = GROUP // P
+CHUNK_TILES = 2
+CHUNK = CHUNK_TILES * P
+CHUNKS = [(g, b, h) for g in range(GROUPS) for b in range(BATCH) for h in range(TILES // CHUNK_TILES)]
+DOWN, UP, ROPE = range(3)
+
+RATIO = 10000.0 ** (-1.0 / HALF)
 TWO_PI = 2.0 * math.pi
-PS = [(1,1),(1,1),(1,1),(0,0)]
-VQ = [(), (), (1,), ()]
+QUARTER_PI = math.pi / 4
+SAFE_ANGLE = 3.1415
+
+VECTOR_CAST_PAIRS = (0, 2, 6, 7)
+VECTOR_UP_CHUNKS = (2, 4)
+VECTOR_ADD_CHUNKS = (13, 14)
 
 
 def reduced_columns(group):
-    last = 512 * group + 511
-    j = 0
-    while last * RHO**j > 3.1415:
-        j += 1
-    return (j + 7) // 8 * 8
+    last = GROUP * (group + 1) - 1
+    count = 0
+    while last * RATIO**count > SAFE_ANGLE:
+        count += 1
+    return (count + 7) // 8 * 8
+
+
+MOST_REDUCED = reduced_columns(GROUPS - 1)
+
+
+def tile_columns(i):
+    return slice(P * i, P * (i + 1))
 
 
 def tile_multiheadlatentattention_pa_t_w4_kernel(
@@ -41,343 +59,365 @@ def tile_multiheadlatentattention_pa_t_w4_kernel(
     nc = tc.nc
     with ExitStack() as ctx:
         keep = ctx.enter_context(tc.tile_pool(name="keep", bufs=1))
-        xin = ctx.enter_context(tc.tile_pool(name="xin", bufs=8))
-        work = ctx.enter_context(tc.tile_pool(name="work", bufs=3))
-        tabs = ctx.enter_context(tc.tile_pool(name="tabs", bufs=3))
-        outs = ctx.enter_context(tc.tile_pool(name="outs", bufs=5))
+        byte_pool = ctx.enter_context(tc.tile_pool(name="byte_pool", bufs=GROUPS * BATCH))
+        work = ctx.enter_context(tc.tile_pool(name="work", bufs=4))
+        table_pool = ctx.enter_context(tc.tile_pool(name="table_pool", bufs=3))
+        out_pool = ctx.enter_context(tc.tile_pool(name="out_pool", bufs=5))
         psum = ctx.enter_context(tc.psum_pool(name="psum", bufs=1))
 
-        x_tiles = {}
+        byte_tiles = {}
 
-        def load_x(g, b):
-            t = xin.tile([P, 4 * D], U8, name="xb")
+        def load_bytes(g, b):
+            tile = byte_pool.tile([P, TILES * WIDTH], U8, name="x_byte_tile")
             nc.sync.dma_start(
-                out=t[:], in_=x_bytes[b, 512 * g : 512 * g + 512, :].rearrange("(p i) k -> p (i k)", i=4)
+                out=tile[:], in_=x_bytes[b, GROUP * g : GROUP * (g + 1), :].rearrange("(p i) k -> p (i k)", i=TILES)
             )
-            x_tiles[(g, b)] = t
+            byte_tiles[(g, b)] = tile
 
-        planes = keep.tile([P, 3, D], U8, name="planes", align_bytes=64)
+        planes = keep.tile([P, 3, WIDTH], U8, name="planes", align_bytes=64)
         nc.gpsimd.memset(planes[:].rearrange("p w n -> p (w n)").bitcast(I32), 0)
 
-        def load_scales(w, scales):
-            for q in range(4):
+        def load_scale_bytes(place, scales):
+            for quadrant in range(4):
                 nc.sync.dma_start(
-                    out=planes[32 * q : 32 * q + 4, w, :].bitcast(I32),
-                    in_=scales[0, 4 * q : 4 * q + 4, :].bitcast(I32),
+                    out=planes[32 * quadrant : 32 * quadrant + 4, place, :].bitcast(I32),
+                    in_=scales[0, 4 * quadrant : 4 * quadrant + 4, :].bitcast(I32),
                 )
 
+        down_raw = keep.tile([P, 2 * WIDTH], U8, name="down_raw", align_bytes=64)
+        up_codes = keep.tile([P, 2 * WIDTH], U8, name="up_codes", align_bytes=64)
+        rope_codes = keep.tile([P, 2 * WIDTH], U8, name="rope_codes", align_bytes=64)
         x_factor = keep.tile([P, 1, 2, 2], F32, name="x_factor")
-        down_raw = keep.tile([P, 2 * D], U8, name="down_raw", align_bytes=64)
-        up_codes = keep.tile([P, 2 * D], U8, name="up_codes", align_bytes=64)
-        rope_codes = keep.tile([P, 2 * D], U8, name="rope_codes", align_bytes=64)
-        load_x(0, 0)
+        load_bytes(0, 0)
         nc.sync.dma_start(
             out=x_factor[:].rearrange("p o u e -> p (o u e)"), in_=x_scale.rearrange("a o (p t) -> p (a o t)", t=4)
         )
         nc.sync.dma_start(out=down_raw[:], in_=down_words[0])
-        load_scales(0, down_scales)
-        load_x(0, 1)
+        load_scale_bytes(DOWN, down_scales)
+        load_bytes(0, 1)
+        load_bytes(1, 0)
         nc.sync.dma_start(out=rope_codes[:], in_=rope_words[0])
-        load_scales(2, rope_scales)
+        load_scale_bytes(ROPE, rope_scales)
         nc.sync.dma_start(out=up_codes[:], in_=up_words[0])
-        load_scales(1, up_scales)
+        load_scale_bytes(UP, up_scales)
         for g in range(1, GROUPS):
-            for b in range(B):
-                load_x(g, b)
+            for b in range(BATCH):
+                if (g, b) not in byte_tiles:
+                    load_bytes(g, b)
 
-        dummy = keep.tile([P, 1], F32, name="dummy")
-        nc.vector.memset(dummy[:], 0.0)
-        nc.scalar.activation(out=dummy[:], in_=dummy[:], func=ACT.Sin)
-        pos = keep.tile([P, 4 * GROUPS], F32, name="pos")
+        warm = keep.tile([P, 1], F32, name="warm")
+        nc.vector.memset(warm[:], 0.0)
+        nc.scalar.activation(out=warm[:], in_=warm[:], func=ACT.Sin)
+        position = keep.tile([P, GROUPS * TILES], F32, name="position")
         nc.gpsimd.iota(
-            pos[:],
-            pattern=[[512, GROUPS], [1, 4]],
+            position[:],
+            pattern=[[GROUP, GROUPS], [1, TILES]],
             base=0,
-            channel_multiplier=4,
+            channel_multiplier=TILES,
             allow_small_or_imprecise_dtypes=True,
         )
-        freq = keep.tile([P, HALF], F32, name="freq")
-        nc.vector.memset(freq[:], 1.0)
+        frequency = keep.tile([P, HALF], F32, name="frequency")
+        nc.vector.memset(frequency[:], 1.0)
         nc.vector.tensor_scalar(
-            out=freq[:, 0:1], in0=freq[:, 0:1], scalar1=1.0 / TWO_PI, scalar2=None, op0=ALU.mult
+            out=frequency[:, 0:1], in0=frequency[:, 0:1], scalar1=1.0 / TWO_PI, scalar2=None, op0=ALU.mult
         )
-        w = 1
-        while w < HALF:
+        known = 1
+        while known < HALF:
             nc.vector.tensor_scalar(
-                out=freq[:, w : 2 * w], in0=freq[:, 0:w], scalar1=RHO**w, scalar2=None, op0=ALU.mult
+                out=frequency[:, known : 2 * known],
+                in0=frequency[:, 0:known],
+                scalar1=RATIO**known,
+                scalar2=None,
+                op0=ALU.mult,
             )
-            w *= 2
-        ident = keep.tile([P, P], F32, name="ident")
-        make_identity(nc, ident[:])
+            known *= 2
+        identity = keep.tile([P, P], F32, name="identity")
+        make_identity(nc, identity[:])
 
-        turns = keep.tile([P, 4 * GROUPS, HALF], F32, name="turns")
-        whole = keep.tile([P, 4 * GROUPS, 192], I32, name="whole")
+        turns = keep.tile([P, GROUPS * TILES, HALF], F32, name="turns")
+        whole_turns = keep.tile([P, GROUPS * TILES, MOST_REDUCED], I32, name="whole_turns")
 
-        def raw_angles(eng, first, last):
-            for c in range(first, last):
-                j0 = reduced_columns(c // 4)
-                eng.tensor_scalar(
-                    out=whole[:, c, 0:j0], in0=freq[:, 0:j0], scalar1=pos[:, c : c + 1], scalar2=0.0,
-                    op0=ALU.mult, op1=ALU.add,
+        def raw_turns(engine, first, last):
+            for tile in range(first, last):
+                low = reduced_columns(tile // TILES)
+                nc.gpsimd.tensor_scalar(
+                    out=whole_turns[:, tile, 0:low],
+                    in0=frequency[:, 0:low],
+                    scalar1=position[:, tile : tile + 1],
+                    scalar2=0.0,
+                    op0=ALU.mult,
+                    op1=ALU.add,
                 )
-                eng.tensor_scalar(
-                    out=turns[:, c, :], in0=freq[:], scalar1=pos[:, c : c + 1], scalar2=0.0,
-                    op0=ALU.mult, op1=ALU.add,
+                engine.tensor_scalar(
+                    out=turns[:, tile, :],
+                    in0=frequency[:],
+                    scalar1=position[:, tile : tile + 1],
+                    scalar2=0.0,
+                    op0=ALU.mult,
+                    op1=ALU.add,
                 )
 
-        def reduce_angles(first, last):
-            j0 = reduced_columns(first // 4)
-            part = turns[:, first:last, 0:j0]
-            nc.vector.tensor_tensor(out=part, in0=part, in1=whole[:, first:last, 0:j0], op=ALU.subtract)
+        def reduce_turns(first, last):
+            low = reduced_columns(first // TILES)
+            part = turns[:, first:last, 0:low]
+            nc.vector.tensor_tensor(
+                out=part, in0=part, in1=whole_turns[:, first:last, 0:low], op=ALU.subtract
+            )
 
         tables = {}
+        table_work = []
 
-        def table_steps(first, last):
-            g = first // 4
-            j0 = reduced_columns(g)
-            if first % 4 == 0:
-                sin_t = tabs.tile([P, 4, HALF], F32, name="sin_t")
-                mix_t = tabs.tile([P, 4, 2, HALF], F32, name="mix_t")
-                bent = tabs.tile([P, 4, 2, 192], F32, name="bent")
-                tables[g] = (sin_t, mix_t, bent)
-            sin_t, mix_t, bent = tables[g]
-            own = slice(first - 4 * g, last - 4 * g)
-            low, high = turns[:, first:last, 0:j0], turns[:, first:last, j0:HALF]
+        def plan_tables(first, last):
+            g = first // TILES
+            low = reduced_columns(g)
+            if first % TILES == 0:
+                sin_table = table_pool.tile([P, TILES, HALF], F32, name="sin_table")
+                mix_table = table_pool.tile([P, TILES, 2, HALF], F32, name="mix_table")
+                bent = table_pool.tile([P, TILES, 2, MOST_REDUCED], F32, name="bent")
+                tables[g] = (sin_table, mix_table, bent)
+            sin_table, mix_table, bent = tables[g]
+            own = slice(first - TILES * g, last - TILES * g)
+            turns_low, turns_high = turns[:, first:last, 0:low], turns[:, first:last, low:HALF]
+            for destination, source, func, bias, scale in (
+                (mix_table[:, own, 0, low:HALF], turns_high, ACT.Sin, 3 * QUARTER_PI, -TWO_PI),
+                (mix_table[:, own, 1, low:HALF], turns_high, ACT.Sin, QUARTER_PI, -TWO_PI),
+                (bent[:, own, 0, 0:low], turns_low, ACT.Abs, -QUARTER_PI, TWO_PI),
+                (bent[:, own, 1, 0:low], turns_low, ACT.Abs, QUARTER_PI, TWO_PI),
+                (mix_table[:, own, :, 0:low], bent[:, own, :, 0:low], ACT.Sin, 2 * QUARTER_PI, -1.0),
+                (sin_table[:, own, :], turns[:, first:last, :], ACT.Sin, 0.0, TWO_PI),
+            ):
+                table_work.append((destination, source, func, bias, scale))
 
-            def act(o, i, f, bias, scale):
-                return lambda: nc.scalar.activation(out=o, in_=i, func=f, bias=bias, scale=scale)
-
-            q = math.pi / 4
-            return [
-                act(bent[:, own, 0, 0:j0], low, ACT.Abs, -q, TWO_PI),
-                act(bent[:, own, 1, 0:j0], low, ACT.Abs, q, TWO_PI),
-                act(mix_t[:, own, 0, j0:HALF], high, ACT.Sin, 3 * q, -TWO_PI),
-                act(mix_t[:, own, 1, j0:HALF], high, ACT.Sin, q, -TWO_PI),
-                act(mix_t[:, own, :, 0:j0], bent[:, own, :, 0:j0], ACT.Sin, 2 * q, -1.0),
-                act(sin_t[:, own, :], turns[:, first:last, :], ACT.Sin, 0.0, TWO_PI),
-            ]
+        def make_tables(count):
+            for step in range(min(count, len(table_work))):
+                destination, source, func, bias, scale = table_work.pop(0)
+                nc.scalar.activation(out=destination, in_=source, func=func, bias=bias, scale=scale)
 
         down_codes = keep.tile([P, 4, 2 * P], U8, name="down_codes", align_bytes=64)
         down_plane = keep.tile([P, 4, P], U8, name="down_plane", align_bytes=64)
 
-        chunks = [(g, b, h) for g in range(GROUPS) for b in range(B) for h in range(2)]
-        n = len(chunks)
-        xw, xg, xq, lg, lq = {}, {}, {}, {}, {}
-        stages, mixes, sines, u_banks = {}, {}, {}, {}
+        def regroup_down():
+            nc.vector.tensor_copy(
+                out=down_codes[:].rearrange("p t (m b) -> p t m b", b=2),
+                in_=down_raw[:].rearrange("p (m t b) -> p t m b", t=4, b=2),
+            )
+            nc.vector.tensor_copy(out=down_plane[:], in_=planes[:, DOWN, :].rearrange("p (m t) -> p t m", t=4))
 
-        def cols(i):
-            return slice(P * i, P * (i + 1))
+        wide, word_banks, x_grouped, x_quantised = {}, {}, {}, {}
+        latent_grouped, latent_quantised, sum_banks = {}, {}, {}
+        mixed_tiles, sined_tiles, stages = {}, {}, {}
 
-        def widen(copy, first, last):
-            g, b, h = chunks[first]
+        def widen(first, last):
+            g, b, h = CHUNKS[first]
+            pair = first // 2
             if h == 0:
-                xw[first // 2] = work.tile([P, 2, 2 * D], BF16, name="xw", align_bytes=64)
+                wide[pair] = work.tile([P, 2, CHUNK_TILES * WIDTH], BF16, name="wide", align_bytes=64)
+            span = CHUNK_TILES * WIDTH
+            copy = nc.vector.tensor_copy if pair in VECTOR_CAST_PAIRS else nc.scalar.copy
             copy(
-                out=xw[first // 2][:, h : h + last - first, :].rearrange("p c k -> p (c k)"),
-                in_=x_tiles[(g, b)][:, 2 * D * h : 2 * D * (h + last - first)].bitcast(FP8),
+                out=wide[pair][:, h : h + last - first, :].rearrange("p c k -> p (c k)"),
+                in_=byte_tiles[(g, b)][:, span * h : span * (h + last - first)].bitcast(FP8),
             )
 
-        def turn(c):
-            words = xw[c // 2][:, c % 2, :].bitcast(F32)
-            bank = psum.tile([P, 2, 2 * P], F32, name="u_bank" if c in (1, 3) else "xt_bank")
-            for i in range(2):
+        def flip(c):
+            words = wide[c // 2][:, c % 2, :].bitcast(F32)
+            bank = psum.tile([P, 2, CHUNK], F32, name="sum_bank" if c in (1, 3) else "word_bank")
+            row = WIDTH // 2
+            for i in range(CHUNK_TILES):
                 for u in range(2):
-                    nc.tensor.transpose(bank[:, u, cols(i)], words[:, 256 * i + u : 256 * (i + 1) : 2], ident[:])
+                    nc.tensor.transpose(bank[:, u, tile_columns(i)], words[:, row * i + u : row * (i + 1) : 2], identity[:])
+            word_banks[c] = bank
+
+        def rescale(c):
             if c % 2 == 0:
-                xg[c // 2] = work.tile([P, 2, 4 * 256], BF16, name="xg", align_bytes=64)
+                x_grouped[c // 2] = work.tile([P, 2, 4 * CHUNK], BF16, name="x_grouped", align_bytes=64)
             nc.vector.tensor_tensor(
-                out=xg[c // 2][:, c % 2, :].rearrange("p (r u e) -> p r u e", u=2, e=2),
-                in0=bank[:].bitcast(BF16).rearrange("p u (r e) -> p r u e", e=2),
-                in1=x_factor[:].to_broadcast([P, 256, 2, 2]),
+                out=x_grouped[c // 2][:, c % 2, :].rearrange("p (n u e) -> p n u e", u=2, e=2),
+                in0=word_banks[c][:].bitcast(BF16).rearrange("p u (n e) -> p n u e", e=2),
+                in1=x_factor[:].to_broadcast([P, CHUNK, 2, 2]),
                 op=ALU.mult,
             )
 
-        def quant_x(first, last):
+        def quantise_x(first, last):
             h = first % 2
             if h == 0:
-                codes = work.tile([P, 2, 256], U32, name="x_codes", align_bytes=64)
-                plane = work.tile([P, 2, 256], U8, name="x_plane", align_bytes=64)
-                xq[first // 2] = (codes, plane)
-            codes, plane = xq[first // 2]
+                codes = work.tile([P, 2, CHUNK], U32, name="x_codes", align_bytes=64)
+                plane = work.tile([P, 2, CHUNK], U8, name="x_plane", align_bytes=64)
+                x_quantised[first // 2] = (codes, plane)
+            codes, plane = x_quantised[first // 2]
             own = slice(h, h + last - first)
             nc.vector.quantize_mx(
                 out=codes[:, own, :].rearrange("p c n -> p (c n)").bitcast(FP8X4),
                 scales=plane[:, own, :].rearrange("p c n -> p (c n)"),
-                in_=xg[first // 2][:, own, :].rearrange("p c n -> p (c n)"),
+                in_=x_grouped[first // 2][:, own, :].rearrange("p c n -> p (c n)"),
             )
 
         def latent(c):
-            codes, plane = xq[c // 2]
-            lg[c] = work.tile([P, 4 * 256], BF16, name="lg", align_bytes=64)
-            for i in range(2):
-                bank = psum.tile([P, 4, P], F32, name="lat_bank%d" % i)
+            codes, plane = x_quantised[c // 2]
+            latent_grouped[c] = work.tile([P, CHUNK_TILES, 4 * P], BF16, name="latent_grouped", align_bytes=64)
+            for i in range(CHUNK_TILES):
+                bank = psum.tile([P, 4, P], F32, name="latent_bank%d" % i)
                 for t in range(4):
                     nc.tensor.matmul_mx(
                         out=bank[:, t, :],
                         lhsT=down_codes[:, t, :].bitcast(FP4X4),
                         lhsT_scale=down_plane[:, t, :],
-                        rhs=codes[:, c % 2, cols(i)].bitcast(FP8X4),
-                        rhs_scale=plane[:, c % 2, cols(i)],
+                        rhs=codes[:, c % 2, tile_columns(i)].bitcast(FP8X4),
+                        rhs_scale=plane[:, c % 2, tile_columns(i)],
                         start=True,
                         stop=True,
                     )
                 nc.scalar.copy(
-                    out=lg[c][:, 512 * i : 512 * (i + 1)].rearrange("p (n t) -> p n t", t=4),
-                    in_=bank[:].rearrange("p t n -> p n t"),
+                    out=latent_grouped[c][:, i, :].rearrange("p (m j t) -> p m t j", j=4, t=4),
+                    in_=bank[:].rearrange("p t (m j) -> p m t j", j=4),
                 )
 
-        def quant_latent(c):
-            codes = work.tile([P, 256], U32, name="l_codes", align_bytes=64)
-            plane = work.tile([P, 256], U8, name="l_plane", align_bytes=64)
-            nc.vector.quantize_mx(out=codes[:].bitcast(FP8X4), scales=plane[:], in_=lg[c][:])
-            lq[c] = (codes, plane)
+        def quantise_latent(c):
+            codes = work.tile([P, CHUNK], U32, name="latent_codes", align_bytes=64)
+            plane = work.tile([P, CHUNK], U8, name="latent_plane", align_bytes=64)
+            nc.vector.quantize_mx(
+                out=codes[:].bitcast(FP8X4), scales=plane[:], in_=latent_grouped[c][:].rearrange("p i n -> p (i n)")
+            )
+            latent_quantised[c] = (codes, plane)
 
-        def mm(c, i, o, words, pl, a, count, start, stop):
-            codes, plane = lq[c]
+        def multiply(c, i, destination, words, place, column, count, start, stop):
+            codes, plane = latent_quantised[c]
             nc.tensor.matmul_mx(
-                out=o,
-                lhsT=codes[:, cols(i)].bitcast(FP8X4),
-                lhsT_scale=plane[:, cols(i)],
-                rhs=words[:, 2 * a : 2 * (a + count)].bitcast(FP4X4),
-                rhs_scale=planes[:, pl, a : a + count],
+                out=destination,
+                lhsT=codes[:, tile_columns(i)].bitcast(FP8X4),
+                lhsT_scale=plane[:, tile_columns(i)],
+                rhs=words[:, 2 * column : 2 * (column + count)].bitcast(FP4X4),
+                rhs_scale=planes[:, place, column : column + count],
                 start=start,
                 stop=stop,
             )
 
         def project_rope(c):
-            g, b, h = chunks[c]
-            stages[c] = outs.tile([P, 2, H, 256], F32, name="stage")
-            mixes[c] = work.tile([P, 2, D], F32, name="mixed")
-            sines[c] = work.tile([P, 2, HALF], F32, name="sined")
-            for i in range(2):
-                r_bank = psum.tile([P, D], F32, name="r_bank%d" % i)
-                mm(c, i, r_bank[:], rope_codes, 2, 0, D, True, True)
+            g, b, h = CHUNKS[c]
+            mix_table = tables[g][1]
+            mixed_tiles[c] = work.tile([P, CHUNK_TILES, WIDTH], F32, name="mixed")
+            for i in range(CHUNK_TILES):
+                bank = psum.tile([P, WIDTH], F32, name="rope_bank%d" % i)
+                multiply(c, i, bank[:], rope_codes, ROPE, 0, WIDTH, True, True)
                 nc.vector.scalar_tensor_tensor(
-                    out=mixes[c][:, i, :], in0=r_bank[:], scalar=math.sqrt(2.0),
-                    in1=tables[g][1][:, 2 * h + i, :, :].rearrange("p s c -> p (s c)"),
-                    op0=ALU.mult, op1=ALU.mult,
+                    out=mixed_tiles[c][:, i, :],
+                    in0=bank[:],
+                    scalar=math.sqrt(2.0),
+                    in1=mix_table[:, CHUNK_TILES * h + i, :, :].rearrange("p s c -> p (s c)"),
+                    op0=ALU.mult,
+                    op1=ALU.mult,
                 )
 
         def project_up(c):
-            for i in range(2):
-                q_bank = psum.tile([P, D], F32, name="q_bank%d" % i)
-                mm(c, i, q_bank[:], up_codes, 1, 0, D, True, True)
-                copy = nc.vector.tensor_copy if i in VQ[c % 4] else nc.scalar.copy
-                copy(out=stages[c][:, i, :, 0:P], in_=q_bank[:].rearrange("p (h c) -> p h c", h=H))
+            stages[c] = out_pool.tile([P, CHUNK_TILES, HEADS, 2 * P], F32, name="stage")
+            for i in range(CHUNK_TILES):
+                bank = psum.tile([P, WIDTH], F32, name="up_bank%d" % i)
+                multiply(c, i, bank[:], up_codes, UP, 0, WIDTH, True, True)
+                copy = nc.vector.tensor_copy if i == 1 and c in VECTOR_UP_CHUNKS else nc.scalar.copy
+                copy(out=stages[c][:, i, :, 0:P], in_=bank[:].rearrange("p (h c) -> p h c", h=HEADS))
 
         def project_sum(c):
-            u_banks[c] = psum.tile([P, 2, HALF], F32, name="u_bank")
-            for i in range(2):
-                for half in range(2):
-                    o = u_banks[c][:, i, P * half : P * (half + 1)]
-                    mm(c, i, o, rope_codes, 2, P * half, P, True, False)
-                    mm(c, i, o, rope_codes, 2, HALF + P * half, P, False, True)
+            sum_banks[c] = psum.tile([P, CHUNK_TILES, HALF], F32, name="sum_bank")
+            for i in range(CHUNK_TILES):
+                for column in range(0, HALF, P):
+                    destination = sum_banks[c][:, i, column : column + P]
+                    multiply(c, i, destination, rope_codes, ROPE, column, P, True, False)
+                    multiply(c, i, destination, rope_codes, ROPE, HALF + column, P, False, True)
 
-        def sine_part(c):
-            g, b, h = chunks[c]
+        def times_sine(c, first, last):
+            g, b, h = CHUNKS[c]
+            if first == 0:
+                sined_tiles[c] = work.tile([P, CHUNK_TILES, HALF], F32, name="sined")
+            sin_table = tables[g][0]
             nc.vector.tensor_tensor(
-                out=sines[c][:], in0=u_banks[c][:], in1=tables[g][0][:, 2 * h : 2 * h + 2, :], op=ALU.mult
+                out=sined_tiles[c][:, first:last, :],
+                in0=sum_banks[c][:, first:last, :],
+                in1=sin_table[:, CHUNK_TILES * h + first : CHUNK_TILES * h + last, :],
+                op=ALU.mult,
             )
 
-        def combine(eng, c, head, op):
-            eng.tensor_tensor(
-                out=stages[c][:, :, head : head + 2, P:256],
-                in0=mixes[c][:].rearrange("p i (h c) -> p i h c", h=H)[:, :, head : head + 2, :],
-                in1=sines[c][:].rearrange("p i (h c) -> p i h c", h=2),
-                op=op,
+        def add_half(engine, c, first, last, half):
+            heads = slice(2 * half, 2 * half + 2)
+            engine.tensor_tensor(
+                out=stages[c][:, first:last, heads, P : 2 * P],
+                in0=mixed_tiles[c][:, first:last, :].rearrange("p i (h c) -> p i h c", h=HEADS)[:, :, heads, :],
+                in1=sined_tiles[c][:, first:last, :].rearrange("p i (h c) -> p i h c", h=2),
+                op=ALU.add if half else ALU.subtract,
             )
 
-        def store(c):
-            g, b, h = chunks[c]
-            rows = out[b, 512 * g : 512 * g + 512, :, :].rearrange("(p i) h c -> p i h c", i=4)
-            nc.sync.dma_start(out=rows[:, 2 * h : 2 * h + 2], in_=stages[c][:])
-
-        def last_chunk(c):
-            g, b, h = chunks[c]
-            rows = out[b, 512 * g : 512 * g + 512, :, :].rearrange("(p i) h c -> p i h c", i=4)
-            for i in range(2):
-                nc.vector.tensor_tensor(
-                    out=sines[c][:, i, :], in0=u_banks[c][:, i, :], in1=tables[g][0][:, 2 * h + i, :], op=ALU.mult
-                )
-            for i in range(2):
-                for eng, head, op in ((nc.vector, 0, ALU.subtract), (nc.gpsimd, 2, ALU.add)):
-                    eng.tensor_tensor(
-                        out=stages[c][:, i, head : head + 2, P:256],
-                        in0=mixes[c][:, i, :].rearrange("p (h c) -> p h c", h=H)[:, head : head + 2, :],
-                        in1=sines[c][:, i, :].rearrange("p (h c) -> p h c", h=2),
-                        op=op,
-                    )
-                nc.sync.dma_start(out=rows[:, 2 * h + i], in_=stages[c][:, i])
-
-        def prepare_down():
-            nc.vector.tensor_copy(
-                out=down_codes[:].rearrange("p t (m b) -> p t m b", b=2),
-                in_=down_raw[:].rearrange("p (m t b) -> p t m b", t=4, b=2),
-            )
-            nc.vector.tensor_copy(
-                out=down_plane[:], in_=planes[:, 0, :].rearrange("p (m t) -> p t m", t=4)
+        def store(c, first, last):
+            g, b, h = CHUNKS[c]
+            rows = out[b, GROUP * g : GROUP * (g + 1), :, :].rearrange("(p i) h c -> p i h c", i=TILES)
+            nc.sync.dma_start(
+                out=rows[:, CHUNK_TILES * h + first : CHUNK_TILES * h + last], in_=stages[c][:, first:last]
             )
 
-        pieces = []
-
-        def table_piece(count):
-            for i in range(count):
-                if pieces:
-                    pieces.pop(0)()
-
+        last_chunk = len(CHUNKS) - 1
         with tc.manual_schedule():
-            raw_angles(nc.vector, 0, 2)
-            widen(nc.vector.tensor_copy, 0, 1)
-            reduce_angles(0, 2)
-            raw_angles(nc.gpsimd, 2, 16)
-            pieces.extend(table_steps(0, 2))
-            widen(nc.vector.tensor_copy, 1, 2)
-            table_piece(2)
-            widen(nc.scalar.copy, 2, 4)
-            prepare_down()
-            turn(0)
-            reduce_angles(2, 4)
-            table_piece(4)
-            pieces.extend(table_steps(2, 4))
-            quant_x(0, 1)
-            turn(1)
+            plan_tables(0, 2)
+            raw_turns(nc.vector, 0, 2)
+            make_tables(2)
+            widen(0, 1)
+            reduce_turns(0, 2)
+            raw_turns(nc.gpsimd, 2, GROUPS * TILES)
+            flip(0)
+            widen(1, 2)
+            rescale(0)
+            flip(1)
+            make_tables(2)
+            widen(2, 4)
+            quantise_x(0, 1)
+            flip(2)
+            regroup_down()
+            rescale(1)
             latent(0)
-            table_piece(2)
-            quant_x(1, 2)
-            turn(2)
-            widen(nc.scalar.copy, 4, 6)
+            make_tables(1)
+            quantise_x(1, 2)
+            rescale(2)
+            flip(3)
+            reduce_turns(2, 4)
+            plan_tables(2, 4)
+            make_tables(len(table_work))
             latent(1)
-            table_piece(2)
-            quant_latent(0)
-            turn(3)
-            quant_x(2, 4)
-            reduce_angles(4, 8)
-            table_piece(2)
-            pieces.extend(table_steps(4, 8))
-            for k in range(n):
-                project_rope(k)
-                if k + 4 < n:
-                    turn(k + 4)
-                project_up(k)
-                table_piece(PS[k % 4][0])
-                project_sum(k)
-                if k + 2 < n:
-                    latent(k + 2)
-                if k + 1 < n:
-                    quant_latent(k + 1)
-                if k % 2 == 1 and k + 3 < n:
-                    quant_x(k + 3, k + 5)
-                if k in (1, 5):
-                    reduce_angles(k + 7, k + 11)
-                if k == n - 1:
-                    last_chunk(k)
-                else:
-                    sine_part(k)
-                    combine(nc.vector if k >= n - 2 else nc.gpsimd, k, 0, ALU.subtract)
-                    combine(nc.gpsimd, k, 2, ALU.add)
-                    store(k)
-                if k % 2 == 0 and k + 6 < n:
-                    widen(nc.scalar.copy, k + 6, k + 8)
-                if k % 4 == 3 and (k + 1) // 4 + 1 < GROUPS:
-                    pieces.extend(table_steps(k + 5, k + 9))
-                table_piece(PS[k % 4][1])
+            quantise_latent(0)
+            widen(4, 6)
+            rescale(3)
+            quantise_x(2, 4)
+            reduce_turns(TILES, 2 * TILES)
+            plan_tables(TILES, 2 * TILES)
+
+            for c in range(len(CHUNKS)):
+                g, phase = divmod(c, 4)
+                project_rope(c)
+                if c + 4 <= last_chunk:
+                    flip(c + 4)
+                    rescale(c + 4)
+                project_up(c)
+                make_tables(1)
+                project_sum(c)
+                if c + 2 <= last_chunk:
+                    latent(c + 2)
+                if c + 1 <= last_chunk:
+                    quantise_latent(c + 1)
+                if c % 2 == 1 and c + 3 <= last_chunk:
+                    quantise_x(c + 3, c + 5)
+                if phase == 1 and g + 2 < GROUPS:
+                    reduce_turns(TILES * (g + 2), TILES * (g + 3))
+                if c < last_chunk:
+                    times_sine(c, 0, CHUNK_TILES)
+                    add_half(nc.vector if c in VECTOR_ADD_CHUNKS else nc.gpsimd, c, 0, CHUNK_TILES, 0)
+                    add_half(nc.gpsimd, c, 0, CHUNK_TILES, 1)
+                    store(c, 0, CHUNK_TILES)
+                if c % 2 == 0 and c + 6 <= last_chunk:
+                    widen(c + 6, c + 8)
+                if phase == 3 and g + 2 < GROUPS:
+                    plan_tables(TILES * (g + 2), TILES * (g + 3))
+                if phase < 2:
+                    make_tables(1)
+
+            for i in range(CHUNK_TILES):
+                times_sine(last_chunk, i, i + 1)
+            for i in range(CHUNK_TILES):
+                add_half(nc.vector, last_chunk, i, i + 1, 0)
+                add_half(nc.gpsimd, last_chunk, i, i + 1, 1)
+                store(last_chunk, i, i + 1)

import math
from contextlib import ExitStack

import concourse.mybir as mybir
from concourse.masks import make_identity

F32 = mybir.dt.float32
BF16 = mybir.dt.bfloat16
I32 = mybir.dt.int32
U32 = mybir.dt.uint32
U8 = mybir.dt.uint8
FP8 = mybir.dt.float8_e4m3fn
FP8X4 = mybir.dt.float8_e4m3fn_x4
FP4X4 = mybir.dt.float4_e2m1fn_x4
ALU = mybir.AluOpType
ACT = mybir.ActivationFunctionType

BATCH, SEQ, WIDTH, HEADS = 2, 2048, 512, 4
FLOPS = 3 * 2 * BATCH * SEQ * WIDTH * WIDTH

P = 128
HALF = WIDTH // 2
GROUP = 512
GROUPS = SEQ // GROUP
TILES = GROUP // P
CHUNK_TILES = 2
CHUNK = CHUNK_TILES * P
CHUNKS = [(g, b, h) for g in range(GROUPS) for b in range(BATCH) for h in range(TILES // CHUNK_TILES)]
DOWN, UP, ROPE = range(3)

RATIO = 10000.0 ** (-1.0 / HALF)
TWO_PI = 2.0 * math.pi
QUARTER_PI = math.pi / 4
SAFE_ANGLE = 3.1415

VECTOR_CAST_PAIRS = (0, 2, 6, 7)
VECTOR_UP_CHUNKS = (2, 4)
VECTOR_ADD_CHUNKS = (13, 14)


def reduced_columns(group):
    last = GROUP * (group + 1) - 1
    count = 0
    while last * RATIO**count > SAFE_ANGLE:
        count += 1
    return (count + 7) // 8 * 8


MOST_REDUCED = reduced_columns(GROUPS - 1)


def tile_columns(i):
    return slice(P * i, P * (i + 1))


def tile_multiheadlatentattention_pa_t_w4_kernel(
    tc, x_bytes, x_scale, down_words, down_scales, up_words, up_scales, rope_words, rope_scales, out
):
    nc = tc.nc
    with ExitStack() as ctx:
        keep = ctx.enter_context(tc.tile_pool(name="keep", bufs=1))
        byte_pool = ctx.enter_context(tc.tile_pool(name="byte_pool", bufs=GROUPS * BATCH))
        work = ctx.enter_context(tc.tile_pool(name="work", bufs=4))
        table_pool = ctx.enter_context(tc.tile_pool(name="table_pool", bufs=3))
        out_pool = ctx.enter_context(tc.tile_pool(name="out_pool", bufs=5))
        psum = ctx.enter_context(tc.psum_pool(name="psum", bufs=1))

        byte_tiles = {}

        def load_bytes(g, b):
            tile = byte_pool.tile([P, TILES * WIDTH], U8, name="x_byte_tile")
            nc.sync.dma_start(
                out=tile[:], in_=x_bytes[b, GROUP * g : GROUP * (g + 1), :].rearrange("(p i) k -> p (i k)", i=TILES)
            )
            byte_tiles[(g, b)] = tile

        planes = keep.tile([P, 3, WIDTH], U8, name="planes", align_bytes=64)
        nc.gpsimd.memset(planes[:].rearrange("p w n -> p (w n)").bitcast(I32), 0)

        def load_scale_bytes(place, scales):
            for quadrant in range(4):
                nc.sync.dma_start(
                    out=planes[32 * quadrant : 32 * quadrant + 4, place, :].bitcast(I32),
                    in_=scales[0, 4 * quadrant : 4 * quadrant + 4, :].bitcast(I32),
                )

        down_raw = keep.tile([P, 2 * WIDTH], U8, name="down_raw", align_bytes=64)
        up_codes = keep.tile([P, 2 * WIDTH], U8, name="up_codes", align_bytes=64)
        rope_codes = keep.tile([P, 2 * WIDTH], U8, name="rope_codes", align_bytes=64)
        x_factor = keep.tile([P, 1, 2, 2], F32, name="x_factor")
        load_bytes(0, 0)
        nc.sync.dma_start(
            out=x_factor[:].rearrange("p o u e -> p (o u e)"), in_=x_scale.rearrange("a o (p t) -> p (a o t)", t=4)
        )
        nc.sync.dma_start(out=down_raw[:], in_=down_words[0])
        load_scale_bytes(DOWN, down_scales)
        load_bytes(0, 1)
        load_bytes(1, 0)
        nc.sync.dma_start(out=rope_codes[:], in_=rope_words[0])
        load_scale_bytes(ROPE, rope_scales)
        nc.sync.dma_start(out=up_codes[:], in_=up_words[0])
        load_scale_bytes(UP, up_scales)
        for g in range(1, GROUPS):
            for b in range(BATCH):
                if (g, b) not in byte_tiles:
                    load_bytes(g, b)

        warm = keep.tile([P, 1], F32, name="warm")
        nc.vector.memset(warm[:], 0.0)
        nc.scalar.activation(out=warm[:], in_=warm[:], func=ACT.Sin)
        position = keep.tile([P, GROUPS * TILES], F32, name="position")
        nc.gpsimd.iota(
            position[:],
            pattern=[[GROUP, GROUPS], [1, TILES]],
            base=0,
            channel_multiplier=TILES,
            allow_small_or_imprecise_dtypes=True,
        )
        frequency = keep.tile([P, HALF], F32, name="frequency")
        nc.vector.memset(frequency[:], 1.0)
        nc.vector.tensor_scalar(
            out=frequency[:, 0:1], in0=frequency[:, 0:1], scalar1=1.0 / TWO_PI, scalar2=None, op0=ALU.mult
        )
        known = 1
        while known < HALF:
            nc.vector.tensor_scalar(
                out=frequency[:, known : 2 * known],
                in0=frequency[:, 0:known],
                scalar1=RATIO**known,
                scalar2=None,
                op0=ALU.mult,
            )
            known *= 2
        identity = keep.tile([P, P], F32, name="identity")
        make_identity(nc, identity[:])

        turns = keep.tile([P, GROUPS * TILES, HALF], F32, name="turns")
        whole_turns = keep.tile([P, GROUPS * TILES, MOST_REDUCED], I32, name="whole_turns")

        def raw_turns(engine, first, last):
            for tile in range(first, last):
                low = reduced_columns(tile // TILES)
                nc.gpsimd.tensor_scalar(
                    out=whole_turns[:, tile, 0:low],
                    in0=frequency[:, 0:low],
                    scalar1=position[:, tile : tile + 1],
                    scalar2=0.0,
                    op0=ALU.mult,
                    op1=ALU.add,
                )
                engine.tensor_scalar(
                    out=turns[:, tile, :],
                    in0=frequency[:],
                    scalar1=position[:, tile : tile + 1],
                    scalar2=0.0,
                    op0=ALU.mult,
                    op1=ALU.add,
                )

        def reduce_turns(first, last):
            low = reduced_columns(first // TILES)
            part = turns[:, first:last, 0:low]
            nc.vector.tensor_tensor(
                out=part, in0=part, in1=whole_turns[:, first:last, 0:low], op=ALU.subtract
            )

        tables = {}
        table_work = []

        def plan_tables(first, last):
            g = first // TILES
            low = reduced_columns(g)
            if first % TILES == 0:
                sin_table = table_pool.tile([P, TILES, HALF], F32, name="sin_table")
                mix_table = table_pool.tile([P, TILES, 2, HALF], F32, name="mix_table")
                bent = table_pool.tile([P, TILES, 2, MOST_REDUCED], F32, name="bent")
                tables[g] = (sin_table, mix_table, bent)
            sin_table, mix_table, bent = tables[g]
            own = slice(first - TILES * g, last - TILES * g)
            turns_low, turns_high = turns[:, first:last, 0:low], turns[:, first:last, low:HALF]
            for destination, source, func, bias, scale in (
                (mix_table[:, own, 0, low:HALF], turns_high, ACT.Sin, 3 * QUARTER_PI, -TWO_PI),
                (mix_table[:, own, 1, low:HALF], turns_high, ACT.Sin, QUARTER_PI, -TWO_PI),
                (bent[:, own, 0, 0:low], turns_low, ACT.Abs, -QUARTER_PI, TWO_PI),
                (bent[:, own, 1, 0:low], turns_low, ACT.Abs, QUARTER_PI, TWO_PI),
                (mix_table[:, own, :, 0:low], bent[:, own, :, 0:low], ACT.Sin, 2 * QUARTER_PI, -1.0),
                (sin_table[:, own, :], turns[:, first:last, :], ACT.Sin, 0.0, TWO_PI),
            ):
                table_work.append((destination, source, func, bias, scale))

        def make_tables(count):
            for step in range(min(count, len(table_work))):
                destination, source, func, bias, scale = table_work.pop(0)
                nc.scalar.activation(out=destination, in_=source, func=func, bias=bias, scale=scale)

        down_codes = keep.tile([P, 4, 2 * P], U8, name="down_codes", align_bytes=64)
        down_plane = keep.tile([P, 4, P], U8, name="down_plane", align_bytes=64)

        def regroup_down():
            nc.vector.tensor_copy(
                out=down_codes[:].rearrange("p t (m b) -> p t m b", b=2),
                in_=down_raw[:].rearrange("p (m t b) -> p t m b", t=4, b=2),
            )
            nc.vector.tensor_copy(out=down_plane[:], in_=planes[:, DOWN, :].rearrange("p (m t) -> p t m", t=4))

        wide, word_banks, x_grouped, x_quantised = {}, {}, {}, {}
        latent_grouped, latent_quantised, sum_banks = {}, {}, {}
        mixed_tiles, sined_tiles, stages = {}, {}, {}

        def widen(first, last):
            g, b, h = CHUNKS[first]
            pair = first // 2
            if h == 0:
                wide[pair] = work.tile([P, 2, CHUNK_TILES * WIDTH], BF16, name="wide", align_bytes=64)
            span = CHUNK_TILES * WIDTH
            copy = nc.vector.tensor_copy if pair in VECTOR_CAST_PAIRS else nc.scalar.copy
            copy(
                out=wide[pair][:, h : h + last - first, :].rearrange("p c k -> p (c k)"),
                in_=byte_tiles[(g, b)][:, span * h : span * (h + last - first)].bitcast(FP8),
            )

        def flip(c):
            words = wide[c // 2][:, c % 2, :].bitcast(F32)
            bank = psum.tile([P, 2, CHUNK], F32, name="sum_bank" if c in (1, 3) else "word_bank")
            row = WIDTH // 2
            for i in range(CHUNK_TILES):
                for u in range(2):
                    nc.tensor.transpose(bank[:, u, tile_columns(i)], words[:, row * i + u : row * (i + 1) : 2], identity[:])
            word_banks[c] = bank

        def rescale(c):
            if c % 2 == 0:
                x_grouped[c // 2] = work.tile([P, 2, 4 * CHUNK], BF16, name="x_grouped", align_bytes=64)
            nc.vector.tensor_tensor(
                out=x_grouped[c // 2][:, c % 2, :].rearrange("p (n u e) -> p n u e", u=2, e=2),
                in0=word_banks[c][:].bitcast(BF16).rearrange("p u (n e) -> p n u e", e=2),
                in1=x_factor[:].to_broadcast([P, CHUNK, 2, 2]),
                op=ALU.mult,
            )

        def quantise_x(first, last):
            h = first % 2
            if h == 0:
                codes = work.tile([P, 2, CHUNK], U32, name="x_codes", align_bytes=64)
                plane = work.tile([P, 2, CHUNK], U8, name="x_plane", align_bytes=64)
                x_quantised[first // 2] = (codes, plane)
            codes, plane = x_quantised[first // 2]
            own = slice(h, h + last - first)
            nc.vector.quantize_mx(
                out=codes[:, own, :].rearrange("p c n -> p (c n)").bitcast(FP8X4),
                scales=plane[:, own, :].rearrange("p c n -> p (c n)"),
                in_=x_grouped[first // 2][:, own, :].rearrange("p c n -> p (c n)"),
            )

        def latent(c):
            codes, plane = x_quantised[c // 2]
            latent_grouped[c] = work.tile([P, CHUNK_TILES, 4 * P], BF16, name="latent_grouped", align_bytes=64)
            for i in range(CHUNK_TILES):
                bank = psum.tile([P, 4, P], F32, name="latent_bank%d" % i)
                for t in range(4):
                    nc.tensor.matmul_mx(
                        out=bank[:, t, :],
                        lhsT=down_codes[:, t, :].bitcast(FP4X4),
                        lhsT_scale=down_plane[:, t, :],
                        rhs=codes[:, c % 2, tile_columns(i)].bitcast(FP8X4),
                        rhs_scale=plane[:, c % 2, tile_columns(i)],
                        start=True,
                        stop=True,
                    )
                nc.scalar.copy(
                    out=latent_grouped[c][:, i, :].rearrange("p (m j t) -> p m t j", j=4, t=4),
                    in_=bank[:].rearrange("p t (m j) -> p m t j", j=4),
                )

        def quantise_latent(c):
            codes = work.tile([P, CHUNK], U32, name="latent_codes", align_bytes=64)
            plane = work.tile([P, CHUNK], U8, name="latent_plane", align_bytes=64)
            nc.vector.quantize_mx(
                out=codes[:].bitcast(FP8X4), scales=plane[:], in_=latent_grouped[c][:].rearrange("p i n -> p (i n)")
            )
            latent_quantised[c] = (codes, plane)

        def multiply(c, i, destination, words, place, column, count, start, stop):
            codes, plane = latent_quantised[c]
            nc.tensor.matmul_mx(
                out=destination,
                lhsT=codes[:, tile_columns(i)].bitcast(FP8X4),
                lhsT_scale=plane[:, tile_columns(i)],
                rhs=words[:, 2 * column : 2 * (column + count)].bitcast(FP4X4),
                rhs_scale=planes[:, place, column : column + count],
                start=start,
                stop=stop,
            )

        def project_rope(c):
            g, b, h = CHUNKS[c]
            mix_table = tables[g][1]
            mixed_tiles[c] = work.tile([P, CHUNK_TILES, WIDTH], F32, name="mixed")
            for i in range(CHUNK_TILES):
                bank = psum.tile([P, WIDTH], F32, name="rope_bank%d" % i)
                multiply(c, i, bank[:], rope_codes, ROPE, 0, WIDTH, True, True)
                nc.vector.scalar_tensor_tensor(
                    out=mixed_tiles[c][:, i, :],
                    in0=bank[:],
                    scalar=math.sqrt(2.0),
                    in1=mix_table[:, CHUNK_TILES * h + i, :, :].rearrange("p s c -> p (s c)"),
                    op0=ALU.mult,
                    op1=ALU.mult,
                )

        def project_up(c):
            stages[c] = out_pool.tile([P, CHUNK_TILES, HEADS, 2 * P], F32, name="stage")
            for i in range(CHUNK_TILES):
                bank = psum.tile([P, WIDTH], F32, name="up_bank%d" % i)
                multiply(c, i, bank[:], up_codes, UP, 0, WIDTH, True, True)
                copy = nc.vector.tensor_copy if i == 1 and c in VECTOR_UP_CHUNKS else nc.scalar.copy
                copy(out=stages[c][:, i, :, 0:P], in_=bank[:].rearrange("p (h c) -> p h c", h=HEADS))

        def project_sum(c):
            sum_banks[c] = psum.tile([P, CHUNK_TILES, HALF], F32, name="sum_bank")
            for i in range(CHUNK_TILES):
                for column in range(0, HALF, P):
                    destination = sum_banks[c][:, i, column : column + P]
                    multiply(c, i, destination, rope_codes, ROPE, column, P, True, False)
                    multiply(c, i, destination, rope_codes, ROPE, HALF + column, P, False, True)

        def times_sine(c, first, last):
            g, b, h = CHUNKS[c]
            if first == 0:
                sined_tiles[c] = work.tile([P, CHUNK_TILES, HALF], F32, name="sined")
            sin_table = tables[g][0]
            nc.vector.tensor_tensor(
                out=sined_tiles[c][:, first:last, :],
                in0=sum_banks[c][:, first:last, :],
                in1=sin_table[:, CHUNK_TILES * h + first : CHUNK_TILES * h + last, :],
                op=ALU.mult,
            )

        def add_half(engine, c, first, last, half):
            heads = slice(2 * half, 2 * half + 2)
            engine.tensor_tensor(
                out=stages[c][:, first:last, heads, P : 2 * P],
                in0=mixed_tiles[c][:, first:last, :].rearrange("p i (h c) -> p i h c", h=HEADS)[:, :, heads, :],
                in1=sined_tiles[c][:, first:last, :].rearrange("p i (h c) -> p i h c", h=2),
                op=ALU.add if half else ALU.subtract,
            )

        def store(c, first, last):
            g, b, h = CHUNKS[c]
            rows = out[b, GROUP * g : GROUP * (g + 1), :, :].rearrange("(p i) h c -> p i h c", i=TILES)
            nc.sync.dma_start(
                out=rows[:, CHUNK_TILES * h + first : CHUNK_TILES * h + last], in_=stages[c][:, first:last]
            )

        last_chunk = len(CHUNKS) - 1
        with tc.manual_schedule():
            plan_tables(0, 2)
            raw_turns(nc.vector, 0, 2)
            make_tables(2)
            widen(0, 1)
            reduce_turns(0, 2)
            raw_turns(nc.gpsimd, 2, GROUPS * TILES)
            flip(0)
            widen(1, 2)
            rescale(0)
            flip(1)
            make_tables(2)
            widen(2, 4)
            quantise_x(0, 1)
            flip(2)
            regroup_down()
            rescale(1)
            latent(0)
            make_tables(1)
            quantise_x(1, 2)
            rescale(2)
            flip(3)
            reduce_turns(2, 4)
            plan_tables(2, 4)
            make_tables(len(table_work))
            latent(1)
            quantise_latent(0)
            widen(4, 6)
            rescale(3)
            quantise_x(2, 4)
            reduce_turns(TILES, 2 * TILES)
            plan_tables(TILES, 2 * TILES)

            for c in range(len(CHUNKS)):
                g, phase = divmod(c, 4)
                project_rope(c)
                if c + 4 <= last_chunk:
                    flip(c + 4)
                    rescale(c + 4)
                project_up(c)
                make_tables(1)
                project_sum(c)
                if c + 2 <= last_chunk:
                    latent(c + 2)
                if c + 1 <= last_chunk:
                    quantise_latent(c + 1)
                if c % 2 == 1 and c + 3 <= last_chunk:
                    quantise_x(c + 3, c + 5)
                if phase == 1 and g + 2 < GROUPS:
                    reduce_turns(TILES * (g + 2), TILES * (g + 3))
                if c < last_chunk:
                    times_sine(c, 0, CHUNK_TILES)
                    add_half(nc.vector if c in VECTOR_ADD_CHUNKS else nc.gpsimd, c, 0, CHUNK_TILES, 0)
                    add_half(nc.gpsimd, c, 0, CHUNK_TILES, 1)
                    store(c, 0, CHUNK_TILES)
                if c % 2 == 0 and c + 6 <= last_chunk:
                    widen(c + 6, c + 8)
                if phase == 3 and g + 2 < GROUPS:
                    plan_tables(TILES * (g + 2), TILES * (g + 3))
                if phase < 2:
                    make_tables(1)

            for i in range(CHUNK_TILES):
                times_sine(last_chunk, i, i + 1)
            for i in range(CHUNK_TILES):
                add_half(nc.vector, last_chunk, i, i + 1, 0)
                add_half(nc.gpsimd, last_chunk, i, i + 1, 1)
                store(last_chunk, i, i + 1)
